import numpy as np
import ml_dtypes


def mxq(x, axis, fmt="e4m3"):
    dtype, down = {"e4m3": (ml_dtypes.float8_e4m3fn, 7), "e5m2": (ml_dtypes.float8_e5m2, 14)}[fmt]
    v = np.moveaxis(np.asarray(x, np.float32).astype(ml_dtypes.bfloat16).astype(np.float64), axis, -1)
    blocks = v.reshape(v.shape[:-1] + (-1, 32))
    amax = np.abs(blocks).max(-1, keepdims=True)
    byte = np.maximum(np.where(amax > 0, np.frexp(amax)[1] - 1 + 127, 0) - down, 1)
    scale = np.exp2(byte - 127.0)
    codes = (blocks / scale).astype(np.float32).astype(dtype).astype(np.float64)
    return np.moveaxis((codes * scale).reshape(v.shape), -1, axis)


WIDE = False


def mx_kscale(k):
    if not WIDE:
        return np.ones(k)
    levels = np.array([10, -10, 5, -5, 0])
    a = np.random.permutation(np.resize(levels, k // 512 * 4)).reshape(k // 512, 4)
    idx = np.arange(k)
    return np.exp2(a[idx // 512, idx % 128 // 32])


BF16 = ml_dtypes.bfloat16


def bf(x):
    return np.asarray(x, np.float32).astype(BF16)


def f64(x):
    return np.asarray(x).astype(np.float64)


B, N, H, DH, E, W, DQ, DKV = 1, 1024, 4, 128, 2, 256, 1024, 1024
DV = E * DH
DM = H * DV
NEG = -3.4028234663852886e38


def silu(v):
    return v / (1.0 + np.exp(-v))


def split_heads(t):
    return t.reshape(B, N, H, DV).transpose(0, 2, 1, 3)


def setup_inputs():
    s = mx_kscale(DKV)
    return {"q": bf(np.random.standard_normal((B, H, N, DH)) * 1.4),
            "k1": bf(np.random.standard_normal((B, H, N, DH)) * 1.4),
            "key_values_input": bf(np.random.standard_normal((B, N, DKV)) * s),
            "Wv1": bf(np.random.standard_normal((DKV, DM)) * 4.0 / np.sqrt(DKV) / s[:, None]),
            "attn_sink": bf(np.log(N) + 0.5 + 0.5 * np.random.standard_normal(H))}


def reference(q, k1, key_values_input, Wv1, attn_sink):
    v1 = split_heads(mxq(f64(key_values_input), 2, "e4m3") @ mxq(f64(Wv1), 0, "e4m3"))
    sim = f64(q) @ f64(k1).transpose(0, 1, 3, 2) * DH ** -0.5
    idx = np.arange(N)
    mask = (idx[None, :] > idx[:, None]) & (idx[None, :] - idx[:, None] <= W)
    sim = np.where(mask, NEG, sim)
    sink = f64(attn_sink)[None, :, None, None]
    m = np.maximum(sim.max(-1, keepdims=True), sink)
    e = np.exp(sim - m)
    den = e.sum(-1, keepdims=True) + np.exp(sink - m)
    return silu((mxq(e, 3, "e4m3") @ mxq(v1, 2, "e4m3")) / den)

@@ -1,0 +1,351 @@
+from contextlib import ExitStack
+
+import concourse.mybir as mybir
+from concourse.masks import make_identity
+
+BF16 = mybir.dt.bfloat16
+F32 = mybir.dt.float32
+U32 = mybir.dt.uint32
+U8 = mybir.dt.uint8
+FP8X4 = mybir.dt.float8_e4m3fn_x4
+ACT = mybir.ActivationFunctionType
+ALU = mybir.AluOpType
+AXIS = mybir.AxisListType
+
+P = 128
+PACK = 4
+K_PASS = P * PACK
+HEADS = 4
+SEQ = 1024
+HEAD_DIM = 128
+VALUE_DIM = 256
+FEATURES = 1024
+MODEL = HEADS * VALUE_DIM
+BLOCKS = SEQ // P
+KEY_PASSES = SEQ // K_PASS
+FEATURE_PASSES = FEATURES // K_PASS
+BANK = 512
+BANK_BLOCKS = BANK // P
+SCALE = HEAD_DIM**-0.5
+MASKED = -3.0e38
+TILES = HEADS * BLOCKS
+LAG = 3
+W_FIRST = 1
+KV_FIRST = 7
+V_FIRST = 12
+FLOPS = 2 * SEQ * FEATURES * MODEL + 2 * HEADS * SEQ * SEQ * (HEAD_DIM + VALUE_DIM)
+
+
+def tile_attention_pa_kernel(tc, q, k1, key_values_input, Wv1, attn_sink, out):
+    nc = tc.nc
+    with ExitStack() as ctx:
+        const = ctx.enter_context(tc.tile_pool(name="const", bufs=1))
+        keep = ctx.enter_context(tc.tile_pool(name="keep", bufs=1))
+        small = ctx.enter_context(tc.tile_pool(name="small", bufs=4))
+        rows = ctx.enter_context(tc.tile_pool(name="rows", bufs=LAG + 1))
+        stage = ctx.enter_context(tc.tile_pool(name="stage", bufs=3))
+        psum = ctx.enter_context(tc.psum_pool(name="psum", bufs=2))
+        ctx.enter_context(tc.manual_schedule())
+
+        def copy_out(on_scalar, dst, src):
+            if on_scalar:
+                nc.scalar.copy(out=dst, in_=src)
+            else:
+                nc.vector.tensor_copy(out=dst, in_=src)
+
+        q_rows = keep.tile([P, HEADS, BLOCKS, HEAD_DIM], BF16)
+        k_rows = keep.tile([P, HEADS, BLOCKS, HEAD_DIM], BF16)
+        sink_bf = const.tile([P, HEADS], BF16)
+        kv_rows = keep.tile([P, BLOCKS, FEATURES], BF16)
+        w_rows = keep.tile([P, FEATURE_PASSES, PACK, MODEL], BF16)
+
+        def load_head(h):
+            nc.sync.dma_start(out=q_rows[:, h], in_=q[0, h].rearrange("(b p) d -> p b d", p=P))
+            nc.sync.dma_start(out=k_rows[:, h], in_=k1[0, h].rearrange("(b p) d -> p b d", p=P))
+
+        load_head(0)
+        nc.sync.dma_start(out=sink_bf[:], in_=attn_sink.partition_broadcast(P))
+        for g in range(FEATURE_PASSES):
+            nc.sync.dma_start(
+                out=w_rows[:, g].rearrange("p (u e) n -> p u (e n)", e=2),
+                in_=Wv1[g * K_PASS : (g + 1) * K_PASS, :].rearrange("(u p e) n -> p u (e n)", p=P, e=2),
+            )
+        load_head(1)
+        kv_blocks = key_values_input[0].rearrange("(b p) f -> p b f", p=P)
+        half = BLOCKS // 2
+        for c in range(2):
+            nc.sync.dma_start(
+                out=kv_rows[:, c * half : (c + 1) * half, :],
+                in_=kv_blocks[:, c * half : (c + 1) * half, :],
+            )
+        for h in range(2, HEADS):
+            load_head(h)
+
+        warm = const.tile([P, 1], F32)
+        nc.vector.memset(warm[:], 0.0)
+        nc.scalar.activation(out=warm[:], in_=warm[:], func=ACT.Exp)
+        ident_bf = const.tile([P, P], BF16)
+        make_identity(nc, ident_bf[:])
+        ident_f32 = const.tile([P, P], F32)
+        make_identity(nc, ident_f32[:])
+        zero_block = const.tile([P, P], BF16)
+        nc.vector.memset(zero_block[:], 0.0)
+        band_f32 = const.tile([P, 2, P], F32)
+        nc.gpsimd.memset(band_f32[:], 0.0)
+        nc.gpsimd.affine_select(
+            out=band_f32[:, 0, :], in_=band_f32[:, 0, :], compare_op=ALU.is_ge, fill=MASKED,
+            base=0, pattern=[[-1, P]], channel_multiplier=1,
+        )
+        nc.gpsimd.affine_select(
+            out=band_f32[:, 1, :], in_=band_f32[:, 1, :], compare_op=ALU.is_ge, fill=MASKED,
+            base=-1, pattern=[[1, P]], channel_multiplier=-1,
+        )
+        band = const.tile([P, 2, P], BF16)
+        nc.vector.tensor_copy(out=band[:], in_=band_f32[:])
+        sink = const.tile([P, HEADS], F32)
+        nc.vector.tensor_copy(out=sink[:], in_=sink_bf[:])
+        neg_sink = const.tile([P, HEADS], F32)
+        nc.vector.tensor_scalar(out=neg_sink[:], in0=sink_bf[:], scalar1=-1.0, scalar2=None, op0=ALU.mult)
+
+        qT = keep.tile([P, HEADS, SEQ], BF16)
+        kT = keep.tile([P, HEADS, SEQ], BF16)
+        neg_max = keep.tile([P, HEADS * BLOCKS], F32)
+        row_sums = keep.tile([P, HEADS * BLOCKS, 2], F32)
+        sink_e = keep.tile([P, HEADS * BLOCKS], F32)
+        den = keep.tile([P, HEADS * BLOCKS], F32)
+        inv_den = keep.tile([P, HEADS * BLOCKS], F32)
+        e_codes = keep.tile([P, HEADS * BLOCKS, KEY_PASSES * P], U32, align_bytes=64)
+        e_scales = keep.tile([P, HEADS * BLOCKS, KEY_PASSES * P], U8, align_bytes=64)
+        v_codes = keep.tile([P, KEY_PASSES, MODEL], U32, align_bytes=64)
+        v_scales = keep.tile([P, KEY_PASSES, MODEL], U8, align_bytes=64)
+
+        kv_grouped = keep.tile([P, BLOCKS, FEATURE_PASSES, P, 2], F32, align_bytes=64)
+        kv_codes = keep.tile([P, BLOCKS, FEATURE_PASSES * P], U32, align_bytes=64)
+        kv_scales = keep.tile([P, BLOCKS, FEATURE_PASSES * P], U8, align_bytes=64)
+        w_grouped = keep.tile([P, FEATURE_PASSES, MODEL, PACK], BF16, align_bytes=64)
+        w_codes = keep.tile([P, FEATURE_PASSES, MODEL], U32, align_bytes=64)
+        w_scales = keep.tile([P, FEATURE_PASSES, MODEL], U8, align_bytes=64)
+        v_grouped = keep.tile([P, KEY_PASSES, MODEL, PACK], BF16, align_bytes=64)
+        kv_words = kv_rows[:].bitcast(F32)
+
+        def transpose_quarter(h, c):
+            src, dst = ((q_rows, qT), (k_rows, kT))[c // 2]
+            first = (c % 2) * BANK_BLOCKS
+            flipped = psum.tile([P, BANK_BLOCKS, P], BF16, tag="work")
+            for b in range(BANK_BLOCKS):
+                nc.tensor.transpose(out=flipped[:, b, :], in_=src[:, h, first + b, :], identity=ident_bf[:])
+            copy_out(c // 2 == 1, dst[:, h, first * P : first * P + BANK], flipped[:].rearrange("p b i -> p (b i)"))
+
+        def live_blocks(ib):
+            return [jb for jb in range(BLOCKS) if jb != ib + 1]
+
+        def bank_widths(ib):
+            return (BANK, (len(live_blocks(ib)) - BANK_BLOCKS) * P)
+
+        banks_of = {}
+        e_rows_of = {}
+        flipped_of = {}
+        grouped_of = {}
+
+        def scores(n):
+            h, ib = divmod(n, BLOCKS)
+            s_lo = psum.tile([P, BANK], F32, tag="s_lo")
+            s_hi = psum.tile([P, BANK], F32, tag="s_hi")
+            banks_of[n] = (s_lo, s_hi)
+            for slot, jb in enumerate(live_blocks(ib)):
+                col = (slot % BANK_BLOCKS) * P
+                dst = banks_of[n][slot // BANK_BLOCKS][:, col : col + P]
+                partly = jb == ib or jb == ib + 2
+                nc.tensor.matmul(
+                    out=dst, lhsT=qT[:, h, ib * P : (ib + 1) * P], rhs=kT[:, h, jb * P : (jb + 1) * P],
+                    start=True, stop=not partly,
+                )
+                if partly:
+                    nc.tensor.matmul(
+                        out=dst, lhsT=ident_bf[:], rhs=band[:, 0 if jb == ib else 1, :], start=False, stop=True
+                    )
+
+        def row_maximum(n):
+            h, ib = divmod(n, BLOCKS)
+            bank_max = small.tile([P, 2], F32)
+            for c in range(2):
+                nc.vector.tensor_reduce(
+                    out=bank_max[:, c : c + 1], in_=banks_of[n][c][:, : bank_widths(ib)[c]], axis=AXIS.X, op=ALU.max
+                )
+            row_max = small.tile([P, 1], F32)
+            nc.vector.tensor_tensor(out=row_max[:], in0=bank_max[:, 0:1], in1=bank_max[:, 1:2], op=ALU.max)
+            nc.vector.tensor_scalar(
+                out=neg_max[:, n : n + 1], in0=row_max[:], scalar1=-SCALE, scalar2=neg_sink[:, h : h + 1],
+                op0=ALU.mult, op1=ALU.min,
+            )
+
+        def exponentials(n):
+            ib = n % BLOCKS
+            e_rows = rows.tile([P, SEQ], BF16)
+            e_rows_of[n] = e_rows
+            for c in range(2):
+                width = bank_widths(ib)[c]
+                nc.scalar.activation(
+                    out=e_rows[:, c * BANK : c * BANK + width], in_=banks_of[n][c][:, :width], func=ACT.Exp,
+                    bias=neg_max[:, n : n + 1], scale=SCALE, accum_out=row_sums[:, n, c : c + 1],
+                )
+
+        def finish_softmax(h):
+            cols = slice(h * BLOCKS, (h + 1) * BLOCKS)
+            nc.scalar.activation(
+                out=sink_e[:, cols], in_=neg_max[:, cols], func=ACT.Exp, bias=sink[:, h : h + 1], scale=1.0
+            )
+            nc.vector.tensor_reduce(out=den[:, cols], in_=row_sums[:, cols, :], axis=AXIS.X, op=ALU.add)
+            nc.vector.tensor_add(out=den[:, cols], in0=den[:, cols], in1=sink_e[:, cols])
+            nc.vector.reciprocal(out=inv_den[:, cols], in_=den[:, cols])
+
+        def flip(n):
+            live = live_blocks(n % BLOCKS)
+            eT_lo = psum.tile([P, PACK, P], BF16, tag="eT_lo", bufs=1)
+            eT_hi = psum.tile([P, PACK, P], BF16, tag="eT_hi", bufs=1)
+            flipped_of[n] = (eT_lo, eT_hi)
+            for jb in range(BLOCKS):
+                if jb in live:
+                    slot = live.index(jb)
+                    src = e_rows_of[n][:, slot * P : (slot + 1) * P]
+                else:
+                    src = zero_block[:]
+                nc.tensor.transpose(out=flipped_of[n][jb // PACK][:, jb % PACK, :], in_=src, identity=ident_bf[:])
+
+        def unload(n, share):
+            grouped = stage.tile([P, KEY_PASSES, P, PACK], BF16, align_bytes=64)
+            grouped_of[n] = grouped
+            for kp in range(KEY_PASSES):
+                copy_out(share and kp == 1, grouped[:, kp], flipped_of[n][kp][:].rearrange("p t i -> p i t"))
+
+        def quantise_e(n):
+            nc.vector.quantize_mx(
+                out=e_codes[:, n, :].bitcast(FP8X4),
+                scales=e_scales[:, n, :],
+                in_=grouped_of[n][:].rearrange("p g i t -> p (g i t)"),
+            )
+
+        def regroup_w(piece):
+            g, c = divmod(piece, MODEL // BANK)
+            cols = slice(c * BANK, (c + 1) * BANK)
+            nc.vector.tensor_copy(
+                out=w_grouped[:, g, cols, :].rearrange("p (c i) t -> p c t i", i=4),
+                in_=w_rows[:, g, :, cols].rearrange("p t (c i) -> p c t i", i=4),
+            )
+
+        def quantise_w(g):
+            nc.vector.quantize_mx(
+                out=w_codes[:, g, :].bitcast(FP8X4),
+                scales=w_scales[:, g, :],
+                in_=w_grouped[:, g].rearrange("p n t -> p (n t)"),
+            )
+
+        def flip_kv(jb):
+            flipped = psum.tile([P, FEATURE_PASSES * 2, P], F32, tag="work")
+            for a in range(FEATURE_PASSES * 2):
+                nc.tensor.transpose(
+                    out=flipped[:, a, :], in_=kv_words[:, jb, a * P : (a + 1) * P], identity=ident_f32[:]
+                )
+            nc.scalar.copy(out=kv_grouped[:, jb], in_=flipped[:].rearrange("p (g u) j -> p g j u", u=2))
+
+        def quantise_kv(jb):
+            nc.vector.quantize_mx(
+                out=kv_codes[:, jb, :].bitcast(FP8X4),
+                scales=kv_scales[:, jb, :],
+                in_=kv_grouped[:].bitcast(BF16)[:, jb].rearrange("p g j t -> p (g j t)"),
+            )
+
+        def project(step):
+            kp, nb = divmod(step, MODEL // P)
+            cols = slice(nb * P, (nb + 1) * P)
+            acc = psum.tile([P, PACK, P], F32, tag="work")
+            for t in range(PACK):
+                jb = kp * PACK + t
+                for g in range(FEATURE_PASSES):
+                    nc.tensor.matmul_mx(
+                        out=acc[:, t, :],
+                        lhsT=kv_codes[:, jb, g * P : (g + 1) * P].bitcast(FP8X4),
+                        lhsT_scale=kv_scales[:, jb, g * P : (g + 1) * P],
+                        rhs=w_codes[:, g, cols].bitcast(FP8X4),
+                        rhs_scale=w_scales[:, g, cols],
+                        start=(g == 0),
+                        stop=(g == FEATURE_PASSES - 1),
+                    )
+            nc.scalar.copy(out=v_grouped[:, kp, cols, :], in_=acc[:].rearrange("p t c -> p c t"))
+
+        def quantise_v(kp):
+            nc.vector.quantize_mx(
+                out=v_codes[:, kp, :].bitcast(FP8X4),
+                scales=v_scales[:, kp, :],
+                in_=v_grouped[:, kp].rearrange("p n t -> p (n t)"),
+            )
+
+        def attend(pair):
+            h, first = divmod(2 * pair, BLOCKS)
+            acc = psum.tile([P, 2, VALUE_DIM], F32, tag="work")
+            result = stage.tile([P, 2, VALUE_DIM], F32)
+            cols = slice(h * VALUE_DIM, (h + 1) * VALUE_DIM)
+            for r in range(2):
+                n = 2 * pair + r
+                for kp in range(KEY_PASSES):
+                    nc.tensor.matmul_mx(
+                        out=acc[:, r, :],
+                        lhsT=e_codes[:, n, kp * P : (kp + 1) * P].bitcast(FP8X4),
+                        lhsT_scale=e_scales[:, n, kp * P : (kp + 1) * P],
+                        rhs=v_codes[:, kp, cols].bitcast(FP8X4),
+                        rhs_scale=v_scales[:, kp, cols],
+                        start=(kp == 0),
+                        stop=(kp == KEY_PASSES - 1),
+                    )
+            for r in range(2):
+                n = 2 * pair + r
+                nc.scalar.activation(
+                    out=result[:, r, :], in_=acc[:, r, :], func=ACT.Silu, scale=inv_den[:, n : n + 1]
+                )
+            nc.sync.dma_start(
+                out=out[0, h, first * P : (first + 2) * P, :].rearrange("(r p) c -> p r c", p=P), in_=result[:]
+            )
+
+        for c in range(4):
+            transpose_quarter(0, c)
+        scores(0)
+        row_maximum(0)
+        for i in range(TILES):
+            h, ib = divmod(i, BLOCKS)
+            if i + 1 < TILES:
+                scores(i + 1)
+            exponentials(i)
+            if i >= LAG:
+                unload(i - LAG, True)
+            if i + 1 < TILES:
+                row_maximum(i + 1)
+            if i >= LAG:
+                quantise_e(i - LAG)
+            if 2 <= ib < 6 and h + 1 < HEADS:
+                transpose_quarter(h + 1, ib - 2)
+            if W_FIRST <= i < W_FIRST + 4:
+                regroup_w(i - W_FIRST)
+            if W_FIRST + 4 <= i < W_FIRST + 4 + FEATURE_PASSES:
+                quantise_w(i - W_FIRST - 4)
+            if KV_FIRST < i <= KV_FIRST + BLOCKS:
+                quantise_kv(i - KV_FIRST - 1)
+            if KV_FIRST <= i < KV_FIRST + BLOCKS:
+                flip_kv(i - KV_FIRST)
+            if V_FIRST < i and (i - V_FIRST) % BLOCKS == 0:
+                quantise_v((i - V_FIRST) // BLOCKS - 1)
+            if V_FIRST <= i < V_FIRST + KEY_PASSES * BLOCKS:
+                project(i - V_FIRST)
+            if i + 1 >= LAG:
+                flip(i + 1 - LAG)
+            if ib == BLOCKS - 1:
+                finish_softmax(h)
+        for j in range(LAG):
+            n = TILES - LAG + j
+            unload(n, False)
+            if j + 1 < LAG:
+                flip(n + 1)
+            quantise_e(n)
+            attend(2 * j)
+            attend(2 * j + 1)
+        for pair in range(2 * LAG, TILES // 2):
+            attend(pair)

@@ -29,7 +29,7 @@ BANK_BLOCKS = BANK // P
 SCALE = HEAD_DIM**-0.5
 MASKED = -3.0e38
 TILES = HEADS * BLOCKS
-LAG = 3
+LAG = 6
 W_FIRST = 1
 KV_FIRST = 7
 V_FIRST = 12
@@ -43,6 +43,7 @@ def tile_attention_pa_kernel(tc, q, k1, key_values_input, Wv1, attn_sink, out):
         keep = ctx.enter_context(tc.tile_pool(name="keep", bufs=1))
         small = ctx.enter_context(tc.tile_pool(name="small", bufs=4))
         rows = ctx.enter_context(tc.tile_pool(name="rows", bufs=LAG + 1))
+        wide = ctx.enter_context(tc.tile_pool(name="wide", bufs=3))
         stage = ctx.enter_context(tc.tile_pool(name="stage", bufs=3))
         psum = ctx.enter_context(tc.psum_pool(name="psum", bufs=2))
         ctx.enter_context(tc.manual_schedule())
@@ -110,7 +111,7 @@ def tile_attention_pa_kernel(tc, q, k1, key_values_input, Wv1, attn_sink, out):
         qT = keep.tile([P, HEADS, SEQ], BF16)
         kT = keep.tile([P, HEADS, SEQ], BF16)
         neg_max = keep.tile([P, HEADS * BLOCKS], F32)
-        row_sums = keep.tile([P, HEADS * BLOCKS, 2], F32)
+        row_sums = keep.tile([P, HEADS * BLOCKS], F32)
         sink_e = keep.tile([P, HEADS * BLOCKS], F32)
         den = keep.tile([P, HEADS * BLOCKS], F32)
         inv_den = keep.tile([P, HEADS * BLOCKS], F32)
@@ -143,6 +144,7 @@ def tile_attention_pa_kernel(tc, q, k1, key_values_input, Wv1, attn_sink, out):
             return (BANK, (len(live_blocks(ib)) - BANK_BLOCKS) * P)
 
         banks_of = {}
+        neg_s_of = {}
         e_rows_of = {}
         flipped_of = {}
         grouped_of = {}
@@ -165,38 +167,39 @@ def tile_attention_pa_kernel(tc, q, k1, key_values_input, Wv1, attn_sink, out):
                         out=dst, lhsT=ident_bf[:], rhs=band[:, 0 if jb == ib else 1, :], start=False, stop=True
                     )
 
-        def row_maximum(n):
+        def shift_out(n, c):
             h, ib = divmod(n, BLOCKS)
-            bank_max = small.tile([P, 2], F32)
-            for c in range(2):
-                nc.vector.tensor_reduce(
-                    out=bank_max[:, c : c + 1], in_=banks_of[n][c][:, : bank_widths(ib)[c]], axis=AXIS.X, op=ALU.max
-                )
-            row_max = small.tile([P, 1], F32)
-            nc.vector.tensor_tensor(out=row_max[:], in0=bank_max[:, 0:1], in1=bank_max[:, 1:2], op=ALU.max)
+            if c == 0:
+                neg_s = wide.tile([P, SEQ], F32)
+                first_min = small.tile([P, 1], F32)
+                neg_m = small.tile([P, 1], F32)
+                neg_s_of[n] = (neg_s, first_min, neg_m)
+            neg_s, first_min, neg_m = neg_s_of[n]
+            width = bank_widths(ib)[c]
             nc.vector.tensor_scalar(
-                out=neg_max[:, n : n + 1], in0=row_max[:], scalar1=-SCALE, scalar2=neg_sink[:, h : h + 1],
-                op0=ALU.mult, op1=ALU.min,
+                out=neg_s[:, c * BANK : c * BANK + width], in0=banks_of[n][c][:, :width], scalar1=-SCALE,
+                scalar2=(neg_sink[:, h : h + 1], first_min[:])[c], op0=ALU.mult, op1=ALU.min,
+                accum_out=(first_min[:], neg_m[:])[c],
             )
 
+        def keep_minimum(n):
+            nc.vector.tensor_copy(out=neg_max[:, n : n + 1], in_=neg_s_of[n][2][:])
+
         def exponentials(n):
-            ib = n % BLOCKS
+            width = sum(bank_widths(n % BLOCKS))
             e_rows = rows.tile([P, SEQ], BF16)
             e_rows_of[n] = e_rows
-            for c in range(2):
-                width = bank_widths(ib)[c]
-                nc.scalar.activation(
-                    out=e_rows[:, c * BANK : c * BANK + width], in_=banks_of[n][c][:, :width], func=ACT.Exp,
-                    bias=neg_max[:, n : n + 1], scale=SCALE, accum_out=row_sums[:, n, c : c + 1],
-                )
+            nc.scalar.activation(
+                out=e_rows[:, :width], in_=neg_s_of[n][0][:, :width], func=ACT.Exp,
+                bias=neg_s_of[n][2][:], scale=-1.0, accum_out=row_sums[:, n : n + 1],
+            )
 
         def finish_softmax(h):
             cols = slice(h * BLOCKS, (h + 1) * BLOCKS)
             nc.scalar.activation(
                 out=sink_e[:, cols], in_=neg_max[:, cols], func=ACT.Exp, bias=sink[:, h : h + 1], scale=1.0
             )
-            nc.vector.tensor_reduce(out=den[:, cols], in_=row_sums[:, cols, :], axis=AXIS.X, op=ALU.add)
-            nc.vector.tensor_add(out=den[:, cols], in0=den[:, cols], in1=sink_e[:, cols])
+            nc.vector.tensor_add(out=den[:, cols], in0=row_sums[:, cols], in1=sink_e[:, cols])
             nc.vector.reciprocal(out=inv_den[:, cols], in_=den[:, cols])
 
         def flip(n):
@@ -212,11 +215,11 @@ def tile_attention_pa_kernel(tc, q, k1, key_values_input, Wv1, attn_sink, out):
                     src = zero_block[:]
                 nc.tensor.transpose(out=flipped_of[n][jb // PACK][:, jb % PACK, :], in_=src, identity=ident_bf[:])
 
-        def unload(n, share):
-            grouped = stage.tile([P, KEY_PASSES, P, PACK], BF16, align_bytes=64)
-            grouped_of[n] = grouped
-            for kp in range(KEY_PASSES):
-                copy_out(share and kp == 1, grouped[:, kp], flipped_of[n][kp][:].rearrange("p t i -> p i t"))
+        def unload(n, kp, on_scalar):
+            if kp == 0:
+                grouped = stage.tile([P, KEY_PASSES, P, PACK], BF16, align_bytes=64)
+                grouped_of[n] = grouped
+            copy_out(on_scalar, grouped_of[n][:, kp], flipped_of[n][kp][:].rearrange("p t i -> p i t"))
 
         def quantise_e(n):
             nc.vector.quantize_mx(
@@ -309,20 +312,26 @@ def tile_attention_pa_kernel(tc, q, k1, key_values_input, Wv1, attn_sink, out):
         for c in range(4):
             transpose_quarter(0, c)
         scores(0)
-        row_maximum(0)
+        scores(1)
+        shift_out(0, 0)
+        shift_out(0, 1)
         for i in range(TILES):
             h, ib = divmod(i, BLOCKS)
+            if i + 2 < TILES:
+                scores(i + 2)
             if i + 1 < TILES:
-                scores(i + 1)
+                shift_out(i + 1, 0)
+            if i >= LAG:
+                unload(i - LAG, 0, False)
+                unload(i - LAG, 1, True)
+            if i + 1 < TILES:
+                shift_out(i + 1, 1)
             exponentials(i)
-            if i >= LAG:
-                unload(i - LAG, True)
-            if i + 1 < TILES:
-                row_maximum(i + 1)
-            if i >= LAG:
-                quantise_e(i - LAG)
-            if 2 <= ib < 6 and h + 1 < HEADS:
-                transpose_quarter(h + 1, ib - 2)
+            if i >= LAG + 1:
+                quantise_e(i - LAG - 1)
+            keep_minimum(i)
+            if 1 <= ib < 5 and h + 1 < HEADS:
+                transpose_quarter(h + 1, ib - 1)
             if W_FIRST <= i < W_FIRST + 4:
                 regroup_w(i - W_FIRST)
             if W_FIRST + 4 <= i < W_FIRST + 4 + FEATURE_PASSES:
@@ -341,11 +350,13 @@ def tile_attention_pa_kernel(tc, q, k1, key_values_input, Wv1, attn_sink, out):
                 finish_softmax(h)
         for j in range(LAG):
             n = TILES - LAG + j
-            unload(n, False)
+            unload(n, 0, False)
+            unload(n, 1, False)
+            quantise_e(n - 1)
             if j + 1 < LAG:
                 flip(n + 1)
-            quantise_e(n)
             attend(2 * j)
             attend(2 * j + 1)
+        quantise_e(TILES - 1)
         for pair in range(2 * LAG, TILES // 2):
             attend(pair)

@@ -29,8 +29,9 @@ BANK_BLOCKS = BANK // P
 SCALE = HEAD_DIM**-0.5
 MASKED = -3.0e38
 TILES = HEADS * BLOCKS
-LAG = 6
+LAG = 8
 W_FIRST = 1
+W_QUANTISE = 8
 KV_FIRST = 7
 V_FIRST = 12
 FLOPS = 2 * SEQ * FEATURES * MODEL + 2 * HEADS * SEQ * SEQ * (HEAD_DIM + VALUE_DIM)
@@ -129,13 +130,11 @@ def tile_attention_pa_kernel(tc, q, k1, key_values_input, Wv1, attn_sink, out):
         v_grouped = keep.tile([P, KEY_PASSES, MODEL, PACK], BF16, align_bytes=64)
         kv_words = kv_rows[:].bitcast(F32)
 
-        def transpose_quarter(h, c):
-            src, dst = ((q_rows, qT), (k_rows, kT))[c // 2]
-            first = (c % 2) * BANK_BLOCKS
-            flipped = psum.tile([P, BANK_BLOCKS, P], BF16, tag="work")
-            for b in range(BANK_BLOCKS):
-                nc.tensor.transpose(out=flipped[:, b, :], in_=src[:, h, first + b, :], identity=ident_bf[:])
-            copy_out(c // 2 == 1, dst[:, h, first * P : first * P + BANK], flipped[:].rearrange("p b i -> p (b i)"))
+        def transpose_rows(h, src, dst):
+            flipped = psum.tile([P, BLOCKS, P], BF16, tag="work")
+            for b in range(BLOCKS):
+                nc.tensor.transpose(out=flipped[:, b, :], in_=src[:, h, b, :], identity=ident_bf[:])
+            nc.vector.tensor_copy(out=dst[:, h, :], in_=flipped[:].rearrange("p b i -> p (b i)"))
 
         def live_blocks(ib):
             return [jb for jb in range(BLOCKS) if jb != ib + 1]
@@ -172,18 +171,14 @@ def tile_attention_pa_kernel(tc, q, k1, key_values_input, Wv1, attn_sink, out):
             if c == 0:
                 neg_s = wide.tile([P, SEQ], F32)
                 first_min = small.tile([P, 1], F32)
-                neg_m = small.tile([P, 1], F32)
-                neg_s_of[n] = (neg_s, first_min, neg_m)
-            neg_s, first_min, neg_m = neg_s_of[n]
+                neg_s_of[n] = (neg_s, first_min)
+            neg_s, first_min = neg_s_of[n]
             width = bank_widths(ib)[c]
             nc.vector.tensor_scalar(
                 out=neg_s[:, c * BANK : c * BANK + width], in0=banks_of[n][c][:, :width], scalar1=-SCALE,
                 scalar2=(neg_sink[:, h : h + 1], first_min[:])[c], op0=ALU.mult, op1=ALU.min,
-                accum_out=(first_min[:], neg_m[:])[c],
+                accum_out=(first_min[:], neg_max[:, n : n + 1])[c],
             )
-
-        def keep_minimum(n):
-            nc.vector.tensor_copy(out=neg_max[:, n : n + 1], in_=neg_s_of[n][2][:])
 
         def exponentials(n):
             width = sum(bank_widths(n % BLOCKS))
@@ -191,49 +186,51 @@ def tile_attention_pa_kernel(tc, q, k1, key_values_input, Wv1, attn_sink, out):
             e_rows_of[n] = e_rows
             nc.scalar.activation(
                 out=e_rows[:, :width], in_=neg_s_of[n][0][:, :width], func=ACT.Exp,
-                bias=neg_s_of[n][2][:], scale=-1.0, accum_out=row_sums[:, n : n + 1],
+                bias=neg_max[:, n : n + 1], scale=-1.0, accum_out=row_sums[:, n : n + 1],
             )
 
-        def finish_softmax(h):
+        def sink_terms(h):
             cols = slice(h * BLOCKS, (h + 1) * BLOCKS)
             nc.scalar.activation(
                 out=sink_e[:, cols], in_=neg_max[:, cols], func=ACT.Exp, bias=sink[:, h : h + 1], scale=1.0
             )
+
+        def denominators(h):
+            cols = slice(h * BLOCKS, (h + 1) * BLOCKS)
             nc.vector.tensor_add(out=den[:, cols], in0=row_sums[:, cols], in1=sink_e[:, cols])
             nc.vector.reciprocal(out=inv_den[:, cols], in_=den[:, cols])
 
         def flip(n):
             live = live_blocks(n % BLOCKS)
-            eT_lo = psum.tile([P, PACK, P], BF16, tag="eT_lo", bufs=1)
-            eT_hi = psum.tile([P, PACK, P], BF16, tag="eT_hi", bufs=1)
-            flipped_of[n] = (eT_lo, eT_hi)
+            eT = psum.tile([P, BLOCKS, P], BF16, tag="eT")
+            flipped_of[n] = eT
             for jb in range(BLOCKS):
                 if jb in live:
                     slot = live.index(jb)
                     src = e_rows_of[n][:, slot * P : (slot + 1) * P]
                 else:
                     src = zero_block[:]
-                nc.tensor.transpose(out=flipped_of[n][jb // PACK][:, jb % PACK, :], in_=src, identity=ident_bf[:])
+                nc.tensor.transpose(out=eT[:, jb, :], in_=src, identity=ident_bf[:])
 
-        def unload(n, kp, on_scalar):
-            if kp == 0:
-                grouped = stage.tile([P, KEY_PASSES, P, PACK], BF16, align_bytes=64)
-                grouped_of[n] = grouped
-            copy_out(on_scalar, grouped_of[n][:, kp], flipped_of[n][kp][:].rearrange("p t i -> p i t"))
+        def unload(n, on_scalar):
+            if n % 2 == 0:
+                grouped = stage.tile([P, 2, KEY_PASSES, P, PACK], BF16, align_bytes=64, bufs=2)
+                grouped_of[n // 2] = grouped
+            copy_out(on_scalar, grouped_of[n // 2][:, n % 2], flipped_of[n][:].rearrange("p (g t) i -> p g i t", t=PACK))
 
-        def quantise_e(n):
+        def quantise_e(pair):
             nc.vector.quantize_mx(
-                out=e_codes[:, n, :].bitcast(FP8X4),
-                scales=e_scales[:, n, :],
-                in_=grouped_of[n][:].rearrange("p g i t -> p (g i t)"),
+                out=e_codes[:, 2 * pair : 2 * pair + 2, :].rearrange("p r w -> p (r w)").bitcast(FP8X4),
+                scales=e_scales[:, 2 * pair : 2 * pair + 2, :].rearrange("p r w -> p (r w)"),
+                in_=grouped_of[pair][:].rearrange("p r g i t -> p (r g i t)"),
             )
 
         def regroup_w(piece):
             g, c = divmod(piece, MODEL // BANK)
             cols = slice(c * BANK, (c + 1) * BANK)
-            nc.vector.tensor_copy(
-                out=w_grouped[:, g, cols, :].rearrange("p (c i) t -> p c t i", i=4),
-                in_=w_rows[:, g, :, cols].rearrange("p t (c i) -> p c t i", i=4),
+            nc.gpsimd.tensor_scalar(
+                out=w_grouped[:, g, cols, :], in0=w_rows[:, g, :, cols].rearrange("p t n -> p n t"),
+                scalar1=1.0, scalar2=0.0, op0=ALU.mult, op1=ALU.add,
             )
 
         def quantise_w(g):
@@ -251,11 +248,12 @@ def tile_attention_pa_kernel(tc, q, k1, key_values_input, Wv1, attn_sink, out):
                 )
             nc.scalar.copy(out=kv_grouped[:, jb], in_=flipped[:].rearrange("p (g u) j -> p g j u", u=2))
 
-        def quantise_kv(jb):
+        def quantise_kv(two):
+            blocks = slice(2 * two, 2 * two + 2)
             nc.vector.quantize_mx(
-                out=kv_codes[:, jb, :].bitcast(FP8X4),
-                scales=kv_scales[:, jb, :],
-                in_=kv_grouped[:].bitcast(BF16)[:, jb].rearrange("p g j t -> p (g j t)"),
+                out=kv_codes[:, blocks, :].rearrange("p b w -> p (b w)").bitcast(FP8X4),
+                scales=kv_scales[:, blocks, :].rearrange("p b w -> p (b w)"),
+                in_=kv_grouped[:].bitcast(BF16)[:, blocks].rearrange("p b g j t -> p (b g j t)"),
             )
 
         def project(step):
@@ -309,54 +307,58 @@ def tile_attention_pa_kernel(tc, q, k1, key_values_input, Wv1, attn_sink, out):
                 out=out[0, h, first * P : (first + 2) * P, :].rearrange("(r p) c -> p r c", p=P), in_=result[:]
             )
 
-        for c in range(4):
-            transpose_quarter(0, c)
+        transpose_rows(0, q_rows, qT)
+        transpose_rows(0, k_rows, kT)
         scores(0)
         scores(1)
         shift_out(0, 0)
         shift_out(0, 1)
         for i in range(TILES):
             h, ib = divmod(i, BLOCKS)
+            packed = i - LAG
             if i + 2 < TILES:
                 scores(i + 2)
             if i + 1 < TILES:
                 shift_out(i + 1, 0)
-            if i >= LAG:
-                unload(i - LAG, 0, False)
-                unload(i - LAG, 1, True)
+            if packed >= 0:
+                unload(packed, packed % 2 == 1)
+            if packed >= 3 and packed % 2 == 1:
+                quantise_e((packed - 3) // 2)
             if i + 1 < TILES:
                 shift_out(i + 1, 1)
             exponentials(i)
-            if i >= LAG + 1:
-                quantise_e(i - LAG - 1)
-            keep_minimum(i)
-            if 1 <= ib < 5 and h + 1 < HEADS:
-                transpose_quarter(h + 1, ib - 1)
+            if ib == 1 and h + 1 < HEADS:
+                transpose_rows(h + 1, q_rows, qT)
+            if ib == 2 and h + 1 < HEADS:
+                transpose_rows(h + 1, k_rows, kT)
             if W_FIRST <= i < W_FIRST + 4:
                 regroup_w(i - W_FIRST)
-            if W_FIRST + 4 <= i < W_FIRST + 4 + FEATURE_PASSES:
-                quantise_w(i - W_FIRST - 4)
-            if KV_FIRST < i <= KV_FIRST + BLOCKS:
-                quantise_kv(i - KV_FIRST - 1)
+            if i in (W_QUANTISE, W_QUANTISE + 2):
+                quantise_w((i - W_QUANTISE) // 2)
+            if KV_FIRST < i <= KV_FIRST + BLOCKS and (i - KV_FIRST) % 2 == 0:
+                quantise_kv((i - KV_FIRST) // 2 - 1)
             if KV_FIRST <= i < KV_FIRST + BLOCKS:
                 flip_kv(i - KV_FIRST)
             if V_FIRST < i and (i - V_FIRST) % BLOCKS == 0:
                 quantise_v((i - V_FIRST) // BLOCKS - 1)
             if V_FIRST <= i < V_FIRST + KEY_PASSES * BLOCKS:
                 project(i - V_FIRST)
-            if i + 1 >= LAG:
-                flip(i + 1 - LAG)
+            if packed + 1 >= 0:
+                flip(packed + 1)
             if ib == BLOCKS - 1:
-                finish_softmax(h)
+                sink_terms(h)
+            if ib == 1 and h > 0:
+                denominators(h - 1)
+        denominators(HEADS - 1)
         for j in range(LAG):
             n = TILES - LAG + j
-            unload(n, 0, False)
-            unload(n, 1, False)
-            quantise_e(n - 1)
+            unload(n, False)
+            if n % 2 == 0:
+                quantise_e(n // 2 - 1)
             if j + 1 < LAG:
                 flip(n + 1)
-            attend(2 * j)
-            attend(2 * j + 1)
-        quantise_e(TILES - 1)
-        for pair in range(2 * LAG, TILES // 2):
+                attend(2 * j)
+                attend(2 * j + 1)
+        quantise_e(TILES // 2 - 1)
+        for pair in range(2 * (LAG - 1), TILES // 2):
             attend(pair)

@@ -34,6 +34,7 @@ W_FIRST = 1
 W_QUANTISE = 8
 KV_FIRST = 7
 V_FIRST = 12
+EARLY = 4
 FLOPS = 2 * SEQ * FEATURES * MODEL + 2 * HEADS * SEQ * SEQ * (HEAD_DIM + VALUE_DIM)
 
 
@@ -134,7 +135,7 @@ def tile_attention_pa_kernel(tc, q, k1, key_values_input, Wv1, attn_sink, out):
             flipped = psum.tile([P, BLOCKS, P], BF16, tag="work")
             for b in range(BLOCKS):
                 nc.tensor.transpose(out=flipped[:, b, :], in_=src[:, h, b, :], identity=ident_bf[:])
-            nc.vector.tensor_copy(out=dst[:, h, :], in_=flipped[:].rearrange("p b i -> p (b i)"))
+            nc.scalar.copy(out=dst[:, h, :], in_=flipped[:].rearrange("p b i -> p (b i)"))
 
         def live_blocks(ib):
             return [jb for jb in range(BLOCKS) if jb != ib + 1]
@@ -281,10 +282,12 @@ def tile_attention_pa_kernel(tc, q, k1, key_values_input, Wv1, attn_sink, out):
                 in_=v_grouped[:, kp].rearrange("p n t -> p (n t)"),
             )
 
-        def attend(pair):
-            h, first = divmod(2 * pair, BLOCKS)
-            acc = psum.tile([P, 2, VALUE_DIM], F32, tag="work")
-            result = stage.tile([P, 2, VALUE_DIM], F32)
+        acc_of = {}
+
+        def weigh(pair):
+            h = 2 * pair // BLOCKS
+            acc = psum.tile([P, 2, VALUE_DIM], F32, tag=("s_lo", "s_hi")[pair % 2] if pair < EARLY else "work")
+            acc_of[pair] = acc
             cols = slice(h * VALUE_DIM, (h + 1) * VALUE_DIM)
             for r in range(2):
                 n = 2 * pair + r
@@ -298,14 +301,23 @@ def tile_attention_pa_kernel(tc, q, k1, key_values_input, Wv1, attn_sink, out):
                         start=(kp == 0),
                         stop=(kp == KEY_PASSES - 1),
                     )
+
+        def finish(pair):
+            h, first = divmod(2 * pair, BLOCKS)
+            result = stage.tile([P, 2, VALUE_DIM], F32)
             for r in range(2):
                 n = 2 * pair + r
                 nc.scalar.activation(
-                    out=result[:, r, :], in_=acc[:, r, :], func=ACT.Silu, scale=inv_den[:, n : n + 1]
+                    out=result[:, r, :], in_=acc_of[pair][:, r, :], func=ACT.Silu, scale=inv_den[:, n : n + 1]
                 )
             nc.sync.dma_start(
                 out=out[0, h, first * P : (first + 2) * P, :].rearrange("(r p) c -> p r c", p=P), in_=result[:]
             )
+
+        def attend(pair):
+            if pair >= EARLY:
+                weigh(pair)
+            finish(pair)
 
         transpose_rows(0, q_rows, qT)
         transpose_rows(0, k_rows, kT)
@@ -350,6 +362,8 @@ def tile_attention_pa_kernel(tc, q, k1, key_values_input, Wv1, attn_sink, out):
             if ib == 1 and h > 0:
                 denominators(h - 1)
         denominators(HEADS - 1)
+        for pair in range(EARLY):
+            weigh(pair)
         for j in range(LAG):
             n = TILES - LAG + j
             unload(n, False)

@@ -44,7 +44,6 @@ def tile_attention_pa_kernel(tc, q, k1, key_values_input, Wv1, attn_sink, out):
         const = ctx.enter_context(tc.tile_pool(name="const", bufs=1))
         keep = ctx.enter_context(tc.tile_pool(name="keep", bufs=1))
         small = ctx.enter_context(tc.tile_pool(name="small", bufs=4))
-        rows = ctx.enter_context(tc.tile_pool(name="rows", bufs=LAG + 1))
         wide = ctx.enter_context(tc.tile_pool(name="wide", bufs=3))
         stage = ctx.enter_context(tc.tile_pool(name="stage", bufs=3))
         psum = ctx.enter_context(tc.psum_pool(name="psum", bufs=2))
@@ -74,12 +73,11 @@ def tile_attention_pa_kernel(tc, q, k1, key_values_input, Wv1, attn_sink, out):
                 in_=Wv1[g * K_PASS : (g + 1) * K_PASS, :].rearrange("(u p e) n -> p u (e n)", p=P, e=2),
             )
         load_head(1)
-        kv_blocks = key_values_input[0].rearrange("(b p) f -> p b f", p=P)
-        half = BLOCKS // 2
-        for c in range(2):
+        kv_blocks = key_values_input[0].rearrange("(c p e) f -> p c (e f)", p=P, e=2)
+        for g in range(KEY_PASSES):
             nc.sync.dma_start(
-                out=kv_rows[:, c * half : (c + 1) * half, :],
-                in_=kv_blocks[:, c * half : (c + 1) * half, :],
+                out=kv_rows[:, g * PACK : (g + 1) * PACK, :].rearrange("p (u e) f -> p u (e f)", e=2),
+                in_=kv_blocks[:, 2 * g : 2 * g + 2, :],
             )
         for h in range(2, HEADS):
             load_head(h)
@@ -91,8 +89,6 @@ def tile_attention_pa_kernel(tc, q, k1, key_values_input, Wv1, attn_sink, out):
         make_identity(nc, ident_bf[:])
         ident_f32 = const.tile([P, P], F32)
         make_identity(nc, ident_f32[:])
-        zero_block = const.tile([P, P], BF16)
-        nc.vector.memset(zero_block[:], 0.0)
         band_f32 = const.tile([P, 2, P], F32)
         nc.gpsimd.memset(band_f32[:], 0.0)
         nc.gpsimd.affine_select(
@@ -130,6 +126,11 @@ def tile_attention_pa_kernel(tc, q, k1, key_values_input, Wv1, attn_sink, out):
         w_scales = keep.tile([P, FEATURE_PASSES, MODEL], U8, align_bytes=64)
         v_grouped = keep.tile([P, KEY_PASSES, MODEL, PACK], BF16, align_bytes=64)
         kv_words = kv_rows[:].bitcast(F32)
+        e_rows = keep.tile([P, BLOCKS, SEQ], BF16)
+        e_words = e_rows[:].bitcast(F32)
+        for ib in range(BLOCKS - 1):
+            hole = (BLOCKS - 1) * P if ib % 2 == 0 else 0
+            nc.gpsimd.memset(e_rows[:, ib, hole : hole + P], 0.0)
 
         def transpose_rows(h, src, dst):
             flipped = psum.tile([P, BLOCKS, P], BF16, tag="work")
@@ -138,14 +139,21 @@ def tile_attention_pa_kernel(tc, q, k1, key_values_input, Wv1, attn_sink, out):
             nc.scalar.copy(out=dst[:, h, :], in_=flipped[:].rearrange("p b i -> p (b i)"))
 
         def live_blocks(ib):
-            return [jb for jb in range(BLOCKS) if jb != ib + 1]
+            if ib == BLOCKS - 1:
+                return list(range(BLOCKS))
+            return [(ib + 2 + slot) % BLOCKS for slot in range(BLOCKS - 1)]
+
+        def ring_start(ib):
+            return (ib + 2 - ib % 2) % BLOCKS
+
+        def first_live(ib):
+            return P if ib % 2 == 1 and ib != BLOCKS - 1 else 0
 
         def bank_widths(ib):
             return (BANK, (len(live_blocks(ib)) - BANK_BLOCKS) * P)
 
         banks_of = {}
         neg_s_of = {}
-        e_rows_of = {}
         flipped_of = {}
         grouped_of = {}
 
@@ -182,11 +190,10 @@ def tile_attention_pa_kernel(tc, q, k1, key_values_input, Wv1, attn_sink, out):
             )
 
         def exponentials(n):
-            width = sum(bank_widths(n % BLOCKS))
-            e_rows = rows.tile([P, SEQ], BF16)
-            e_rows_of[n] = e_rows
+            ib = n % BLOCKS
+            width = sum(bank_widths(ib))
             nc.scalar.activation(
-                out=e_rows[:, :width], in_=neg_s_of[n][0][:, :width], func=ACT.Exp,
+                out=e_rows[:, ib, first_live(ib) : first_live(ib) + width], in_=neg_s_of[n][0][:, :width], func=ACT.Exp,
                 bias=neg_max[:, n : n + 1], scale=-1.0, accum_out=row_sums[:, n : n + 1],
             )
 
@@ -202,28 +209,26 @@ def tile_attention_pa_kernel(tc, q, k1, key_values_input, Wv1, attn_sink, out):
             nc.vector.reciprocal(out=inv_den[:, cols], in_=den[:, cols])
 
         def flip(n):
-            live = live_blocks(n % BLOCKS)
-            eT = psum.tile([P, BLOCKS, P], BF16, tag="eT")
+            ib = n % BLOCKS
+            eT = psum.tile([P, BLOCKS // 2, P], F32, tag="eT")
             flipped_of[n] = eT
-            for jb in range(BLOCKS):
-                if jb in live:
-                    slot = live.index(jb)
-                    src = e_rows_of[n][:, slot * P : (slot + 1) * P]
-                else:
-                    src = zero_block[:]
-                nc.tensor.transpose(out=eT[:, jb, :], in_=src, identity=ident_bf[:])
+            for place in range(BLOCKS // 2):
+                a = (ring_start(ib) // 2 + place) % (BLOCKS // 2)
+                nc.tensor.transpose(
+                    out=eT[:, a, :], in_=e_words[:, ib, place * P : (place + 1) * P], identity=ident_f32[:]
+                )
 
         def unload(n, on_scalar):
             if n % 2 == 0:
-                grouped = stage.tile([P, 2, KEY_PASSES, P, PACK], BF16, align_bytes=64, bufs=2)
+                grouped = stage.tile([P, 2, KEY_PASSES, P, 2], F32, align_bytes=64, bufs=2)
                 grouped_of[n // 2] = grouped
-            copy_out(on_scalar, grouped_of[n // 2][:, n % 2], flipped_of[n][:].rearrange("p (g t) i -> p g i t", t=PACK))
+            copy_out(on_scalar, grouped_of[n // 2][:, n % 2], flipped_of[n][:].rearrange("p (g u) i -> p g i u", u=2))
 
         def quantise_e(pair):
             nc.vector.quantize_mx(
                 out=e_codes[:, 2 * pair : 2 * pair + 2, :].rearrange("p r w -> p (r w)").bitcast(FP8X4),
                 scales=e_scales[:, 2 * pair : 2 * pair + 2, :].rearrange("p r w -> p (r w)"),
-                in_=grouped_of[pair][:].rearrange("p r g i t -> p (r g i t)"),
+                in_=grouped_of[pair][:].bitcast(BF16).rearrange("p r g i t -> p (r g i t)"),
             )
 
         def regroup_w(piece):

@@ -121,10 +121,9 @@ def tile_attention_pa_kernel(tc, q, k1, key_values_input, Wv1, attn_sink, out):
         kv_grouped = keep.tile([P, BLOCKS, FEATURE_PASSES, P, 2], F32, align_bytes=64)
         kv_codes = keep.tile([P, BLOCKS, FEATURE_PASSES * P], U32, align_bytes=64)
         kv_scales = keep.tile([P, BLOCKS, FEATURE_PASSES * P], U8, align_bytes=64)
-        w_grouped = keep.tile([P, FEATURE_PASSES, MODEL, PACK], BF16, align_bytes=64)
+        w_grouped = keep.tile([P, FEATURE_PASSES, MODEL, PACK], BF16, align_bytes=64, tag="grouped")
         w_codes = keep.tile([P, FEATURE_PASSES, MODEL], U32, align_bytes=64)
         w_scales = keep.tile([P, FEATURE_PASSES, MODEL], U8, align_bytes=64)
-        v_grouped = keep.tile([P, KEY_PASSES, MODEL, PACK], BF16, align_bytes=64)
         kv_words = kv_rows[:].bitcast(F32)
         e_rows = keep.tile([P, BLOCKS, SEQ], BF16)
         e_words = e_rows[:].bitcast(F32)
@@ -156,6 +155,7 @@ def tile_attention_pa_kernel(tc, q, k1, key_values_input, Wv1, attn_sink, out):
         neg_s_of = {}
         flipped_of = {}
         grouped_of = {}
+        v_grouped_of = {}
 
         def scores(n):
             h, ib = divmod(n, BLOCKS)
@@ -265,6 +265,10 @@ def tile_attention_pa_kernel(tc, q, k1, key_values_input, Wv1, attn_sink, out):
         def project(step):
             kp, nb = divmod(step, MODEL // P)
             cols = slice(nb * P, (nb + 1) * P)
+            if step == 0:
+                v_grouped = keep.tile([P, KEY_PASSES, MODEL, PACK], BF16, align_bytes=64, tag="grouped")
+                v_grouped_of[0] = v_grouped
+            v_grouped = v_grouped_of[0]
             acc = psum.tile([P, PACK, P], F32, tag="work")
             for t in range(PACK):
                 jb = kp * PACK + t
@@ -284,7 +288,7 @@ def tile_attention_pa_kernel(tc, q, k1, key_values_input, Wv1, attn_sink, out):
             nc.vector.quantize_mx(
                 out=v_codes[:, kp, :].bitcast(FP8X4),
                 scales=v_scales[:, kp, :],
-                in_=v_grouped[:, kp].rearrange("p n t -> p (n t)"),
+                in_=v_grouped_of[0][:, kp].rearrange("p n t -> p (n t)"),
             )
 
         acc_of = {}
@@ -309,7 +313,7 @@ def tile_attention_pa_kernel(tc, q, k1, key_values_input, Wv1, attn_sink, out):
 
         def finish(pair):
             h, first = divmod(2 * pair, BLOCKS)
-            result = stage.tile([P, 2, VALUE_DIM], F32)
+            result = stage.tile([P, 2, VALUE_DIM], F32, bufs=8)
             for r in range(2):
                 n = 2 * pair + r
                 nc.scalar.activation(

@@ -29,12 +29,12 @@ BANK_BLOCKS = BANK // P
 SCALE = HEAD_DIM**-0.5
 MASKED = -3.0e38
 TILES = HEADS * BLOCKS
-LAG = 8
+LAG = 12
 W_FIRST = 1
 W_QUANTISE = 8
 KV_FIRST = 7
 V_FIRST = 12
-EARLY = 4
+AHEAD = 3
 FLOPS = 2 * SEQ * FEATURES * MODEL + 2 * HEADS * SEQ * SEQ * (HEAD_DIM + VALUE_DIM)
 
 
@@ -59,7 +59,7 @@ def tile_attention_pa_kernel(tc, q, k1, key_values_input, Wv1, attn_sink, out):
         k_rows = keep.tile([P, HEADS, BLOCKS, HEAD_DIM], BF16)
         sink_bf = const.tile([P, HEADS], BF16)
         kv_rows = keep.tile([P, BLOCKS, FEATURES], BF16)
-        w_rows = keep.tile([P, FEATURE_PASSES, PACK, MODEL], BF16)
+        w_rows = keep.tile([P, FEATURE_PASSES, PACK, MODEL], BF16, tag="w_then_e")
 
         def load_head(h):
             nc.sync.dma_start(out=q_rows[:, h], in_=q[0, h].rearrange("(b p) d -> p b d", p=P))
@@ -67,12 +67,12 @@ def tile_attention_pa_kernel(tc, q, k1, key_values_input, Wv1, attn_sink, out):
 
         load_head(0)
         nc.sync.dma_start(out=sink_bf[:], in_=attn_sink.partition_broadcast(P))
+        load_head(1)
         for g in range(FEATURE_PASSES):
             nc.sync.dma_start(
                 out=w_rows[:, g].rearrange("p (u e) n -> p u (e n)", e=2),
                 in_=Wv1[g * K_PASS : (g + 1) * K_PASS, :].rearrange("(u p e) n -> p u (e n)", p=P, e=2),
             )
-        load_head(1)
         kv_blocks = key_values_input[0].rearrange("(c p e) f -> p c (e f)", p=P, e=2)
         for g in range(KEY_PASSES):
             nc.sync.dma_start(
@@ -125,11 +125,16 @@ def tile_attention_pa_kernel(tc, q, k1, key_values_input, Wv1, attn_sink, out):
         w_codes = keep.tile([P, FEATURE_PASSES, MODEL], U32, align_bytes=64)
         w_scales = keep.tile([P, FEATURE_PASSES, MODEL], U8, align_bytes=64)
         kv_words = kv_rows[:].bitcast(F32)
-        e_rows = keep.tile([P, BLOCKS, SEQ], BF16)
-        e_words = e_rows[:].bitcast(F32)
-        for ib in range(BLOCKS - 1):
-            hole = (BLOCKS - 1) * P if ib % 2 == 0 else 0
-            nc.gpsimd.memset(e_rows[:, ib, hole : hole + P], 0.0)
+        e_rows_of = {}
+
+        def make_e_rows(which, tag):
+            e_rows = keep.tile([P, BLOCKS, SEQ], BF16, tag=tag)
+            e_rows_of[which] = e_rows
+            for ib in range(BLOCKS - 1):
+                hole = (BLOCKS - 1) * P if ib % 2 == 0 else 0
+                nc.gpsimd.memset(e_rows[:, ib, hole : hole + P], 0.0)
+
+        make_e_rows(0, "e_rows")
 
         def transpose_rows(h, src, dst):
             flipped = psum.tile([P, BLOCKS, P], BF16, tag="work")
@@ -193,7 +198,8 @@ def tile_attention_pa_kernel(tc, q, k1, key_values_input, Wv1, attn_sink, out):
             ib = n % BLOCKS
             width = sum(bank_widths(ib))
             nc.scalar.activation(
-                out=e_rows[:, ib, first_live(ib) : first_live(ib) + width], in_=neg_s_of[n][0][:, :width], func=ACT.Exp,
+                out=e_rows_of[n // BLOCKS % 2][:, ib, first_live(ib) : first_live(ib) + width],
+                in_=neg_s_of[n][0][:, :width], func=ACT.Exp,
                 bias=neg_max[:, n : n + 1], scale=-1.0, accum_out=row_sums[:, n : n + 1],
             )
 
@@ -208,10 +214,11 @@ def tile_attention_pa_kernel(tc, q, k1, key_values_input, Wv1, attn_sink, out):
             nc.vector.tensor_add(out=den[:, cols], in0=row_sums[:, cols], in1=sink_e[:, cols])
             nc.vector.reciprocal(out=inv_den[:, cols], in_=den[:, cols])
 
-        def flip(n):
+        def flip(n, tag="eT"):
             ib = n % BLOCKS
-            eT = psum.tile([P, BLOCKS // 2, P], F32, tag="eT")
+            eT = psum.tile([P, BLOCKS // 2, P], F32, tag=tag)
             flipped_of[n] = eT
+            e_words = e_rows_of[n // BLOCKS % 2][:].bitcast(F32)
             for place in range(BLOCKS // 2):
                 a = (ring_start(ib) // 2 + place) % (BLOCKS // 2)
                 nc.tensor.transpose(
@@ -293,9 +300,9 @@ def tile_attention_pa_kernel(tc, q, k1, key_values_input, Wv1, attn_sink, out):
 
         acc_of = {}
 
-        def weigh(pair):
+        def weigh(pair, tag):
             h = 2 * pair // BLOCKS
-            acc = psum.tile([P, 2, VALUE_DIM], F32, tag=("s_lo", "s_hi")[pair % 2] if pair < EARLY else "work")
+            acc = psum.tile([P, 2, VALUE_DIM], F32, tag=tag)
             acc_of[pair] = acc
             cols = slice(h * VALUE_DIM, (h + 1) * VALUE_DIM)
             for r in range(2):
@@ -323,17 +330,14 @@ def tile_attention_pa_kernel(tc, q, k1, key_values_input, Wv1, attn_sink, out):
                 out=out[0, h, first * P : (first + 2) * P, :].rearrange("(r p) c -> p r c", p=P), in_=result[:]
             )
 
-        def attend(pair):
-            if pair >= EARLY:
-                weigh(pair)
-            finish(pair)
-
         transpose_rows(0, q_rows, qT)
         transpose_rows(0, k_rows, kT)
         scores(0)
         scores(1)
         shift_out(0, 0)
         shift_out(0, 1)
+        transpose_rows(1, q_rows, qT)
+        transpose_rows(1, k_rows, kT)
         for i in range(TILES):
             h, ib = divmod(i, BLOCKS)
             packed = i - LAG
@@ -342,18 +346,20 @@ def tile_attention_pa_kernel(tc, q, k1, key_values_input, Wv1, attn_sink, out):
             if i + 1 < TILES:
                 shift_out(i + 1, 0)
             if packed >= 0:
-                unload(packed, packed % 2 == 1)
+                unload(packed, packed % 2 == 1 or i >= V_FIRST + KEY_PASSES * BLOCKS)
             if packed >= 3 and packed % 2 == 1:
                 quantise_e((packed - 3) // 2)
             if i + 1 < TILES:
                 shift_out(i + 1, 1)
             exponentials(i)
-            if ib == 1 and h + 1 < HEADS:
+            if ib == 1 and 0 < h < HEADS - 1:
                 transpose_rows(h + 1, q_rows, qT)
-            if ib == 2 and h + 1 < HEADS:
+            if ib == 2 and 0 < h < HEADS - 1:
                 transpose_rows(h + 1, k_rows, kT)
             if W_FIRST <= i < W_FIRST + 4:
                 regroup_w(i - W_FIRST)
+            if i == W_FIRST + 4:
+                make_e_rows(1, "w_then_e")
             if i in (W_QUANTISE, W_QUANTISE + 2):
                 quantise_w((i - W_QUANTISE) // 2)
             if KV_FIRST < i <= KV_FIRST + BLOCKS and (i - KV_FIRST) % 2 == 0:
@@ -371,17 +377,27 @@ def tile_attention_pa_kernel(tc, q, k1, key_values_input, Wv1, attn_sink, out):
             if ib == 1 and h > 0:
                 denominators(h - 1)
         denominators(HEADS - 1)
-        for pair in range(EARLY):
-            weigh(pair)
+        flip_tags = ("eT", "s_lo")
+        weigh_tags = ("s_hi", "work")
+        attended = []
+
+        def attend(upto, ready):
+            while len(attended) < min(upto, ready):
+                pair = len(attended)
+                weigh(pair, weigh_tags[pair % 2])
+                finish(pair)
+                attended.append(pair)
+
+        first = TILES - LAG
+        for n in range(first + 1, min(first + AHEAD, TILES)):
+            flip(n, flip_tags[n % 2])
         for j in range(LAG):
-            n = TILES - LAG + j
+            n = first + j
+            if n + AHEAD < TILES:
+                flip(n + AHEAD, flip_tags[(n + AHEAD) % 2])
             unload(n, False)
             if n % 2 == 0:
                 quantise_e(n // 2 - 1)
-            if j + 1 < LAG:
-                flip(n + 1)
-                attend(2 * j)
-                attend(2 * j + 1)
+            attend((j + 1) * (TILES // 2) // LAG + 1, n // 2)
         quantise_e(TILES // 2 - 1)
-        for pair in range(2 * (LAG - 1), TILES // 2):
-            attend(pair)
+        attend(TILES // 2, TILES // 2)

@@ -44,7 +44,7 @@ def tile_attention_pa_kernel(tc, q, k1, key_values_input, Wv1, attn_sink, out):
         const = ctx.enter_context(tc.tile_pool(name="const", bufs=1))
         keep = ctx.enter_context(tc.tile_pool(name="keep", bufs=1))
         small = ctx.enter_context(tc.tile_pool(name="small", bufs=4))
-        wide = ctx.enter_context(tc.tile_pool(name="wide", bufs=3))
+        wide = ctx.enter_context(tc.tile_pool(name="wide", bufs=4))
         stage = ctx.enter_context(tc.tile_pool(name="stage", bufs=3))
         psum = ctx.enter_context(tc.psum_pool(name="psum", bufs=2))
         ctx.enter_context(tc.manual_schedule())
@@ -162,14 +162,12 @@ def tile_attention_pa_kernel(tc, q, k1, key_values_input, Wv1, attn_sink, out):
         grouped_of = {}
         v_grouped_of = {}
 
-        def scores(n):
+        def scores(n, c):
             h, ib = divmod(n, BLOCKS)
-            s_lo = psum.tile([P, BANK], F32, tag="s_lo")
-            s_hi = psum.tile([P, BANK], F32, tag="s_hi")
-            banks_of[n] = (s_lo, s_hi)
-            for slot, jb in enumerate(live_blocks(ib)):
-                col = (slot % BANK_BLOCKS) * P
-                dst = banks_of[n][slot // BANK_BLOCKS][:, col : col + P]
+            bank = psum.tile([P, BANK], F32, tag=("s_lo", "s_hi")[c])
+            banks_of[n, c] = bank
+            for slot, jb in enumerate(live_blocks(ib)[c * BANK_BLOCKS : (c + 1) * BANK_BLOCKS]):
+                dst = bank[:, slot * P : (slot + 1) * P]
                 partly = jb == ib or jb == ib + 2
                 nc.tensor.matmul(
                     out=dst, lhsT=qT[:, h, ib * P : (ib + 1) * P], rhs=kT[:, h, jb * P : (jb + 1) * P],
@@ -189,7 +187,7 @@ def tile_attention_pa_kernel(tc, q, k1, key_values_input, Wv1, attn_sink, out):
             neg_s, first_min = neg_s_of[n]
             width = bank_widths(ib)[c]
             nc.vector.tensor_scalar(
-                out=neg_s[:, c * BANK : c * BANK + width], in0=banks_of[n][c][:, :width], scalar1=-SCALE,
+                out=neg_s[:, c * BANK : c * BANK + width], in0=banks_of[n, c][:, :width], scalar1=-SCALE,
                 scalar2=(neg_sink[:, h : h + 1], first_min[:])[c], op0=ALU.mult, op1=ALU.min,
                 accum_out=(first_min[:], neg_max[:, n : n + 1])[c],
             )
@@ -332,9 +330,12 @@ def tile_attention_pa_kernel(tc, q, k1, key_values_input, Wv1, attn_sink, out):
 
         transpose_rows(0, q_rows, qT)
         transpose_rows(0, k_rows, kT)
-        scores(0)
-        scores(1)
+        for n in range(2):
+            scores(n, 0)
+            scores(n, 1)
         shift_out(0, 0)
+        scores(2, 0)
+        shift_out(1, 0)
         shift_out(0, 1)
         transpose_rows(1, q_rows, qT)
         transpose_rows(1, k_rows, kT)
@@ -342,9 +343,11 @@ def tile_attention_pa_kernel(tc, q, k1, key_values_input, Wv1, attn_sink, out):
             h, ib = divmod(i, BLOCKS)
             packed = i - LAG
             if i + 2 < TILES:
-                scores(i + 2)
-            if i + 1 < TILES:
-                shift_out(i + 1, 0)
+                scores(i + 2, 1)
+            if i + 3 < TILES:
+                scores(i + 3, 0)
+            if i + 2 < TILES:
+                shift_out(i + 2, 0)
             if packed >= 0:
                 unload(packed, packed % 2 == 1 or i >= V_FIRST + KEY_PASSES * BLOCKS)
             if packed >= 3 and packed % 2 == 1:
@@ -376,7 +379,6 @@ def tile_attention_pa_kernel(tc, q, k1, key_values_input, Wv1, attn_sink, out):
                 sink_terms(h)
             if ib == 1 and h > 0:
                 denominators(h - 1)
-        denominators(HEADS - 1)
         flip_tags = ("eT", "s_lo")
         weigh_tags = ("s_hi", "work")
         attended = []
@@ -398,6 +400,8 @@ def tile_attention_pa_kernel(tc, q, k1, key_values_input, Wv1, attn_sink, out):
             unload(n, False)
             if n % 2 == 0:
                 quantise_e(n // 2 - 1)
+            if j == 1:
+                denominators(HEADS - 1)
             attend((j + 1) * (TILES // 2) // LAG + 1, n // 2)
         quantise_e(TILES // 2 - 1)
         attend(TILES // 2, TILES // 2)

@@ -34,7 +34,7 @@ W_FIRST = 1
 W_QUANTISE = 8
 KV_FIRST = 7
 V_FIRST = 12
-AHEAD = 3
+EARLY = 2
 FLOPS = 2 * SEQ * FEATURES * MODEL + 2 * HEADS * SEQ * SEQ * (HEAD_DIM + VALUE_DIM)
 
 
@@ -161,6 +161,7 @@ def tile_attention_pa_kernel(tc, q, k1, key_values_input, Wv1, attn_sink, out):
         flipped_of = {}
         grouped_of = {}
         v_grouped_of = {}
+        projected_of = {}
 
         def scores(n, c):
             h, ib = divmod(n, BLOCKS)
@@ -210,6 +211,9 @@ def tile_attention_pa_kernel(tc, q, k1, key_values_input, Wv1, attn_sink, out):
         def denominators(h):
             cols = slice(h * BLOCKS, (h + 1) * BLOCKS)
             nc.vector.tensor_add(out=den[:, cols], in0=row_sums[:, cols], in1=sink_e[:, cols])
+
+        def invert(h):
+            cols = slice(h * BLOCKS, (h + 1) * BLOCKS)
             nc.vector.reciprocal(out=inv_den[:, cols], in_=den[:, cols])
 
         def flip(n, tag="eT"):
@@ -273,7 +277,6 @@ def tile_attention_pa_kernel(tc, q, k1, key_values_input, Wv1, attn_sink, out):
             if step == 0:
                 v_grouped = keep.tile([P, KEY_PASSES, MODEL, PACK], BF16, align_bytes=64, tag="grouped")
                 v_grouped_of[0] = v_grouped
-            v_grouped = v_grouped_of[0]
             acc = psum.tile([P, PACK, P], F32, tag="work")
             for t in range(PACK):
                 jb = kp * PACK + t
@@ -287,7 +290,14 @@ def tile_attention_pa_kernel(tc, q, k1, key_values_input, Wv1, attn_sink, out):
                         start=(g == 0),
                         stop=(g == FEATURE_PASSES - 1),
                     )
-            nc.scalar.copy(out=v_grouped[:, kp, cols, :], in_=acc[:].rearrange("p t c -> p c t"))
+            projected_of[step] = acc
+
+        def unload_v(step):
+            kp, nb = divmod(step, MODEL // P)
+            cols = slice(nb * P, (nb + 1) * P)
+            nc.scalar.copy(
+                out=v_grouped_of[0][:, kp, cols, :], in_=projected_of[step][:].rearrange("p t c -> p c t")
+            )
 
         def quantise_v(kp):
             nc.vector.quantize_mx(
@@ -328,6 +338,19 @@ def tile_attention_pa_kernel(tc, q, k1, key_values_input, Wv1, attn_sink, out):
                 out=out[0, h, first * P : (first + 2) * P, :].rearrange("(r p) c -> p r c", p=P), in_=result[:]
             )
 
+        attended = []
+
+        def attend(upto, ready):
+            while len(attended) < min(upto, ready):
+                pair = len(attended)
+                if pair >= EARLY:
+                    weigh(pair, ("work", "s_hi")[pair // 2 % 2])
+                finish(pair)
+                attended.append(pair)
+
+        def tail_tag(n):
+            return ("eT", "s_lo")[(n - (TILES - LAG)) // 2 % 2]
+
         transpose_rows(0, q_rows, qT)
         transpose_rows(0, k_rows, kT)
         for n in range(2):
@@ -342,10 +365,9 @@ def tile_attention_pa_kernel(tc, q, k1, key_values_input, Wv1, attn_sink, out):
         for i in range(TILES):
             h, ib = divmod(i, BLOCKS)
             packed = i - LAG
+            step = i - V_FIRST
             if i + 2 < TILES:
                 scores(i + 2, 1)
-            if i + 3 < TILES:
-                scores(i + 3, 0)
             if i + 2 < TILES:
                 shift_out(i + 2, 0)
             if packed >= 0:
@@ -355,6 +377,8 @@ def tile_attention_pa_kernel(tc, q, k1, key_values_input, Wv1, attn_sink, out):
             if i + 1 < TILES:
                 shift_out(i + 1, 1)
             exponentials(i)
+            if 0 < step <= KEY_PASSES * BLOCKS:
+                unload_v(step - 1)
             if ib == 1 and 0 < h < HEADS - 1:
                 transpose_rows(h + 1, q_rows, qT)
             if ib == 2 and 0 < h < HEADS - 1:
@@ -369,39 +393,35 @@ def tile_attention_pa_kernel(tc, q, k1, key_values_input, Wv1, attn_sink, out):
                 quantise_kv((i - KV_FIRST) // 2 - 1)
             if KV_FIRST <= i < KV_FIRST + BLOCKS:
                 flip_kv(i - KV_FIRST)
-            if V_FIRST < i and (i - V_FIRST) % BLOCKS == 0:
-                quantise_v((i - V_FIRST) // BLOCKS - 1)
-            if V_FIRST <= i < V_FIRST + KEY_PASSES * BLOCKS:
-                project(i - V_FIRST)
+            if step > 1 and (step - 1) % BLOCKS == 0:
+                quantise_v((step - 1) // BLOCKS - 1)
             if packed + 1 >= 0:
                 flip(packed + 1)
+            if i + 3 < TILES:
+                scores(i + 3, 0)
+            if 0 <= step < KEY_PASSES * BLOCKS:
+                project(step)
+            if i >= TILES - EARLY:
+                weigh(i - (TILES - EARLY), "work")
             if ib == BLOCKS - 1:
                 sink_terms(h)
             if ib == 1 and h > 0:
                 denominators(h - 1)
-        flip_tags = ("eT", "s_lo")
-        weigh_tags = ("s_hi", "work")
-        attended = []
-
-        def attend(upto, ready):
-            while len(attended) < min(upto, ready):
-                pair = len(attended)
-                weigh(pair, weigh_tags[pair % 2])
-                finish(pair)
-                attended.append(pair)
-
+            if ib == 2 and h > 0:
+                invert(h - 1)
         first = TILES - LAG
-        for n in range(first + 1, min(first + AHEAD, TILES)):
-            flip(n, flip_tags[n % 2])
-        for j in range(LAG):
-            n = first + j
-            if n + AHEAD < TILES:
-                flip(n + AHEAD, flip_tags[(n + AHEAD) % 2])
-            unload(n, False)
-            if n % 2 == 0:
-                quantise_e(n // 2 - 1)
-            if j == 1:
+        flip(first + 1)
+        for a in range(first, TILES, 2):
+            if a + 2 < TILES:
+                flip(a + 2, tail_tag(a + 2))
+                flip(a + 3, tail_tag(a + 3))
+            unload(a, False)
+            quantise_e(a // 2 - 1)
+            unload(a + 1, False)
+            if a == first:
                 denominators(HEADS - 1)
-            attend((j + 1) * (TILES // 2) // LAG + 1, n // 2)
+            if a == first + 2:
+                invert(HEADS - 1)
+            attend((a + 2 - first) * (TILES // 2) // LAG + 1, a // 2)
         quantise_e(TILES // 2 - 1)
         attend(TILES // 2, TILES // 2)

@@ -34,6 +34,8 @@ W_FIRST = 1
 W_QUANTISE = 8
 KV_FIRST = 7
 V_FIRST = 12
+FIRST_Q = 4
+WARM_UP = 4
 EARLY = 2
 FLOPS = 2 * SEQ * FEATURES * MODEL + 2 * HEADS * SEQ * SEQ * (HEAD_DIM + VALUE_DIM)
 
@@ -65,8 +67,11 @@ def tile_attention_pa_kernel(tc, q, k1, key_values_input, Wv1, attn_sink, out):
             nc.sync.dma_start(out=q_rows[:, h], in_=q[0, h].rearrange("(b p) d -> p b d", p=P))
             nc.sync.dma_start(out=k_rows[:, h], in_=k1[0, h].rearrange("(b p) d -> p b d", p=P))
 
-        load_head(0)
+        q_blocks = q[0, 0].rearrange("(b p) d -> p b d", p=P)
+        nc.sync.dma_start(out=q_rows[:, 0, :FIRST_Q], in_=q_blocks[:, :FIRST_Q])
+        nc.sync.dma_start(out=k_rows[:, 0], in_=k1[0, 0].rearrange("(b p) d -> p b d", p=P))
         nc.sync.dma_start(out=sink_bf[:], in_=attn_sink.partition_broadcast(P))
+        nc.sync.dma_start(out=q_rows[:, 0, FIRST_Q:], in_=q_blocks[:, FIRST_Q:])
         load_head(1)
         for g in range(FEATURE_PASSES):
             nc.sync.dma_start(
@@ -85,6 +90,11 @@ def tile_attention_pa_kernel(tc, q, k1, key_values_input, Wv1, attn_sink, out):
         warm = const.tile([P, 1], F32)
         nc.vector.memset(warm[:], 0.0)
         nc.scalar.activation(out=warm[:], in_=warm[:], func=ACT.Exp)
+        zeros = const.tile([P, BANK], BF16)
+        nc.vector.memset(zeros[:], 0.0)
+        for turn in range(WARM_UP):
+            idle = psum.tile([P, BANK], F32, tag="s_hi")
+            nc.tensor.matmul(out=idle[:], lhsT=zeros[:, :P], rhs=zeros[:], start=True, stop=True)
         ident_bf = const.tile([P, P], BF16)
         make_identity(nc, ident_bf[:])
         ident_f32 = const.tile([P, P], F32)
@@ -136,11 +146,12 @@ def tile_attention_pa_kernel(tc, q, k1, key_values_input, Wv1, attn_sink, out):
 
         make_e_rows(0, "e_rows")
 
-        def transpose_rows(h, src, dst):
-            flipped = psum.tile([P, BLOCKS, P], BF16, tag="work")
-            for b in range(BLOCKS):
-                nc.tensor.transpose(out=flipped[:, b, :], in_=src[:, h, b, :], identity=ident_bf[:])
-            nc.scalar.copy(out=dst[:, h, :], in_=flipped[:].rearrange("p b i -> p (b i)"))
+        def transpose_rows(h, src, dst, blocks=(0, BLOCKS), tag="work", on_scalar=True):
+            lo, hi = blocks
+            flipped = psum.tile([P, BLOCKS, P], BF16, tag=tag)
+            for b in range(lo, hi):
+                nc.tensor.transpose(out=flipped[:, b - lo, :], in_=src[:, h, b, :], identity=ident_bf[:])
+            copy_out(on_scalar, dst[:, h, lo * P : hi * P], flipped[:, : hi - lo, :].rearrange("p b i -> p (b i)"))
 
         def live_blocks(ib):
             if ib == BLOCKS - 1:
@@ -334,9 +345,7 @@ def tile_attention_pa_kernel(tc, q, k1, key_values_input, Wv1, attn_sink, out):
                 nc.scalar.activation(
                     out=result[:, r, :], in_=acc_of[pair][:, r, :], func=ACT.Silu, scale=inv_den[:, n : n + 1]
                 )
-            nc.sync.dma_start(
-                out=out[0, h, first * P : (first + 2) * P, :].rearrange("(r p) c -> p r c", p=P), in_=result[:]
-            )
+                nc.sync.dma_start(out=out[0, h, (first + r) * P : (first + r + 1) * P, :], in_=result[:, r, :])
 
         attended = []
 
@@ -351,17 +360,17 @@ def tile_attention_pa_kernel(tc, q, k1, key_values_input, Wv1, attn_sink, out):
         def tail_tag(n):
             return ("eT", "s_lo")[(n - (TILES - LAG)) // 2 % 2]
 
-        transpose_rows(0, q_rows, qT)
-        transpose_rows(0, k_rows, kT)
+        transpose_rows(0, q_rows, qT, (0, FIRST_Q), "work", False)
+        transpose_rows(0, k_rows, kT, (0, BLOCKS // 2), "eT", True)
+        transpose_rows(0, k_rows, kT, (BLOCKS // 2, BLOCKS), "eT", False)
         for n in range(2):
             scores(n, 0)
             scores(n, 1)
+        transpose_rows(0, q_rows, qT, (FIRST_Q, BLOCKS))
         shift_out(0, 0)
         scores(2, 0)
         shift_out(1, 0)
         shift_out(0, 1)
-        transpose_rows(1, q_rows, qT)
-        transpose_rows(1, k_rows, kT)
         for i in range(TILES):
             h, ib = divmod(i, BLOCKS)
             packed = i - LAG
@@ -379,9 +388,9 @@ def tile_attention_pa_kernel(tc, q, k1, key_values_input, Wv1, attn_sink, out):
             exponentials(i)
             if 0 < step <= KEY_PASSES * BLOCKS:
                 unload_v(step - 1)
-            if ib == 1 and 0 < h < HEADS - 1:
+            if ib == 1 and h < HEADS - 1:
                 transpose_rows(h + 1, q_rows, qT)
-            if ib == 2 and 0 < h < HEADS - 1:
+            if ib == 2 and h < HEADS - 1:
                 transpose_rows(h + 1, k_rows, kT)
             if W_FIRST <= i < W_FIRST + 4:
                 regroup_w(i - W_FIRST)

@@ -72,12 +72,13 @@ def tile_attention_pa_kernel(tc, q, k1, key_values_input, Wv1, attn_sink, out):
         nc.sync.dma_start(out=k_rows[:, 0], in_=k1[0, 0].rearrange("(b p) d -> p b d", p=P))
         nc.sync.dma_start(out=sink_bf[:], in_=attn_sink.partition_broadcast(P))
         nc.sync.dma_start(out=q_rows[:, 0, FIRST_Q:], in_=q_blocks[:, FIRST_Q:])
-        load_head(1)
         for g in range(FEATURE_PASSES):
             nc.sync.dma_start(
                 out=w_rows[:, g].rearrange("p (u e) n -> p u (e n)", e=2),
                 in_=Wv1[g * K_PASS : (g + 1) * K_PASS, :].rearrange("(u p e) n -> p u (e n)", p=P, e=2),
             )
+            if g == 0:
+                load_head(1)
         kv_blocks = key_values_input[0].rearrange("(c p e) f -> p c (e f)", p=P, e=2)
         for g in range(KEY_PASSES):
             nc.sync.dma_start(
@@ -92,6 +93,15 @@ def tile_attention_pa_kernel(tc, q, k1, key_values_input, Wv1, attn_sink, out):
         nc.scalar.activation(out=warm[:], in_=warm[:], func=ACT.Exp)
         zeros = const.tile([P, BANK], BF16)
         nc.vector.memset(zeros[:], 0.0)
+        e_rows_of = {}
+
+        def make_e_rows(which, tag, engine):
+            e_rows = keep.tile([P, BLOCKS, SEQ], BF16, tag=tag)
+            e_rows_of[which] = e_rows
+            engine.memset(e_rows[:, 0:BLOCKS:2, (BLOCKS - 1) * P :], 0.0)
+            engine.memset(e_rows[:, 1 : BLOCKS - 1 : 2, :P], 0.0)
+
+        make_e_rows(0, "e_rows", nc.vector)
         for turn in range(WARM_UP):
             idle = psum.tile([P, BANK], F32, tag="s_hi")
             nc.tensor.matmul(out=idle[:], lhsT=zeros[:, :P], rhs=zeros[:], start=True, stop=True)
@@ -135,17 +145,6 @@ def tile_attention_pa_kernel(tc, q, k1, key_values_input, Wv1, attn_sink, out):
         w_codes = keep.tile([P, FEATURE_PASSES, MODEL], U32, align_bytes=64)
         w_scales = keep.tile([P, FEATURE_PASSES, MODEL], U8, align_bytes=64)
         kv_words = kv_rows[:].bitcast(F32)
-        e_rows_of = {}
-
-        def make_e_rows(which, tag):
-            e_rows = keep.tile([P, BLOCKS, SEQ], BF16, tag=tag)
-            e_rows_of[which] = e_rows
-            for ib in range(BLOCKS - 1):
-                hole = (BLOCKS - 1) * P if ib % 2 == 0 else 0
-                nc.gpsimd.memset(e_rows[:, ib, hole : hole + P], 0.0)
-
-        make_e_rows(0, "e_rows")
-
         def transpose_rows(h, src, dst, blocks=(0, BLOCKS), tag="work", on_scalar=True):
             lo, hi = blocks
             flipped = psum.tile([P, BLOCKS, P], BF16, tag=tag)
@@ -388,14 +387,14 @@ def tile_attention_pa_kernel(tc, q, k1, key_values_input, Wv1, attn_sink, out):
             exponentials(i)
             if 0 < step <= KEY_PASSES * BLOCKS:
                 unload_v(step - 1)
-            if ib == 1 and h < HEADS - 1:
+            if ib == 3 and h < HEADS - 1:
                 transpose_rows(h + 1, q_rows, qT)
-            if ib == 2 and h < HEADS - 1:
+            if ib == 4 and h < HEADS - 1:
                 transpose_rows(h + 1, k_rows, kT)
             if W_FIRST <= i < W_FIRST + 4:
                 regroup_w(i - W_FIRST)
             if i == W_FIRST + 4:
-                make_e_rows(1, "w_then_e")
+                make_e_rows(1, "w_then_e", nc.gpsimd)
             if i in (W_QUANTISE, W_QUANTISE + 2):
                 quantise_w((i - W_QUANTISE) // 2)
             if KV_FIRST < i <= KV_FIRST + BLOCKS and (i - KV_FIRST) % 2 == 0:

from contextlib import ExitStack

import concourse.mybir as mybir
from concourse.masks import make_identity

BF16 = mybir.dt.bfloat16
F32 = mybir.dt.float32
U32 = mybir.dt.uint32
U8 = mybir.dt.uint8
FP8X4 = mybir.dt.float8_e4m3fn_x4
ACT = mybir.ActivationFunctionType
ALU = mybir.AluOpType
AXIS = mybir.AxisListType

P = 128
PACK = 4
K_PASS = P * PACK
HEADS = 4
SEQ = 1024
HEAD_DIM = 128
VALUE_DIM = 256
FEATURES = 1024
MODEL = HEADS * VALUE_DIM
BLOCKS = SEQ // P
KEY_PASSES = SEQ // K_PASS
FEATURE_PASSES = FEATURES // K_PASS
BANK = 512
BANK_BLOCKS = BANK // P
SCALE = HEAD_DIM**-0.5
MASKED = -3.0e38
TILES = HEADS * BLOCKS
LAG = 12
W_FIRST = 1
W_QUANTISE = 8
KV_FIRST = 7
V_FIRST = 12
FIRST_Q = 4
WARM_UP = 4
EARLY = 2
FLOPS = 2 * SEQ * FEATURES * MODEL + 2 * HEADS * SEQ * SEQ * (HEAD_DIM + VALUE_DIM)


def tile_attention_pa_kernel(tc, q, k1, key_values_input, Wv1, attn_sink, out):
    nc = tc.nc
    with ExitStack() as ctx:
        const = ctx.enter_context(tc.tile_pool(name="const", bufs=1))
        keep = ctx.enter_context(tc.tile_pool(name="keep", bufs=1))
        small = ctx.enter_context(tc.tile_pool(name="small", bufs=4))
        wide = ctx.enter_context(tc.tile_pool(name="wide", bufs=4))
        stage = ctx.enter_context(tc.tile_pool(name="stage", bufs=3))
        psum = ctx.enter_context(tc.psum_pool(name="psum", bufs=2))
        ctx.enter_context(tc.manual_schedule())

        def copy_out(on_scalar, dst, src):
            if on_scalar:
                nc.scalar.copy(out=dst, in_=src)
            else:
                nc.vector.tensor_copy(out=dst, in_=src)

        q_rows = keep.tile([P, HEADS, BLOCKS, HEAD_DIM], BF16)
        k_rows = keep.tile([P, HEADS, BLOCKS, HEAD_DIM], BF16)
        sink_bf = const.tile([P, HEADS], BF16)
        kv_rows = keep.tile([P, BLOCKS, FEATURES], BF16)
        w_rows = keep.tile([P, FEATURE_PASSES, PACK, MODEL], BF16, tag="w_then_e")

        def load_head(h):
            nc.sync.dma_start(out=q_rows[:, h], in_=q[0, h].rearrange("(b p) d -> p b d", p=P))
            nc.sync.dma_start(out=k_rows[:, h], in_=k1[0, h].rearrange("(b p) d -> p b d", p=P))

        q_blocks = q[0, 0].rearrange("(b p) d -> p b d", p=P)
        nc.sync.dma_start(out=q_rows[:, 0, :FIRST_Q], in_=q_blocks[:, :FIRST_Q])
        nc.sync.dma_start(out=k_rows[:, 0], in_=k1[0, 0].rearrange("(b p) d -> p b d", p=P))
        nc.sync.dma_start(out=sink_bf[:], in_=attn_sink.partition_broadcast(P))
        nc.sync.dma_start(out=q_rows[:, 0, FIRST_Q:], in_=q_blocks[:, FIRST_Q:])
        for g in range(FEATURE_PASSES):
            nc.sync.dma_start(
                out=w_rows[:, g].rearrange("p (u e) n -> p u (e n)", e=2),
                in_=Wv1[g * K_PASS : (g + 1) * K_PASS, :].rearrange("(u p e) n -> p u (e n)", p=P, e=2),
            )
            if g == 0:
                load_head(1)
        kv_blocks = key_values_input[0].rearrange("(c p e) f -> p c (e f)", p=P, e=2)
        for g in range(KEY_PASSES):
            nc.sync.dma_start(
                out=kv_rows[:, g * PACK : (g + 1) * PACK, :].rearrange("p (u e) f -> p u (e f)", e=2),
                in_=kv_blocks[:, 2 * g : 2 * g + 2, :],
            )
        for h in range(2, HEADS):
            load_head(h)

        warm = const.tile([P, 1], F32)
        nc.vector.memset(warm[:], 0.0)
        nc.scalar.activation(out=warm[:], in_=warm[:], func=ACT.Exp)
        zeros = const.tile([P, BANK], BF16)
        nc.vector.memset(zeros[:], 0.0)
        e_rows_of = {}

        def make_e_rows(which, tag, engine):
            e_rows = keep.tile([P, BLOCKS, SEQ], BF16, tag=tag)
            e_rows_of[which] = e_rows
            engine.memset(e_rows[:, 0:BLOCKS:2, (BLOCKS - 1) * P :], 0.0)
            engine.memset(e_rows[:, 1 : BLOCKS - 1 : 2, :P], 0.0)

        make_e_rows(0, "e_rows", nc.vector)
        for turn in range(WARM_UP):
            idle = psum.tile([P, BANK], F32, tag="s_hi")
            nc.tensor.matmul(out=idle[:], lhsT=zeros[:, :P], rhs=zeros[:], start=True, stop=True)
        ident_bf = const.tile([P, P], BF16)
        make_identity(nc, ident_bf[:])
        ident_f32 = const.tile([P, P], F32)
        make_identity(nc, ident_f32[:])
        band_f32 = const.tile([P, 2, P], F32)
        nc.gpsimd.memset(band_f32[:], 0.0)
        nc.gpsimd.affine_select(
            out=band_f32[:, 0, :], in_=band_f32[:, 0, :], compare_op=ALU.is_ge, fill=MASKED,
            base=0, pattern=[[-1, P]], channel_multiplier=1,
        )
        nc.gpsimd.affine_select(
            out=band_f32[:, 1, :], in_=band_f32[:, 1, :], compare_op=ALU.is_ge, fill=MASKED,
            base=-1, pattern=[[1, P]], channel_multiplier=-1,
        )
        band = const.tile([P, 2, P], BF16)
        nc.vector.tensor_copy(out=band[:], in_=band_f32[:])
        sink = const.tile([P, HEADS], F32)
        nc.vector.tensor_copy(out=sink[:], in_=sink_bf[:])
        neg_sink = const.tile([P, HEADS], F32)
        nc.vector.tensor_scalar(out=neg_sink[:], in0=sink_bf[:], scalar1=-1.0, scalar2=None, op0=ALU.mult)

        qT = keep.tile([P, HEADS, SEQ], BF16)
        kT = keep.tile([P, HEADS, SEQ], BF16)
        neg_max = keep.tile([P, HEADS * BLOCKS], F32)
        row_sums = keep.tile([P, HEADS * BLOCKS], F32)
        sink_e = keep.tile([P, HEADS * BLOCKS], F32)
        den = keep.tile([P, HEADS * BLOCKS], F32)
        inv_den = keep.tile([P, HEADS * BLOCKS], F32)
        e_codes = keep.tile([P, HEADS * BLOCKS, KEY_PASSES * P], U32, align_bytes=64)
        e_scales = keep.tile([P, HEADS * BLOCKS, KEY_PASSES * P], U8, align_bytes=64)
        v_codes = keep.tile([P, KEY_PASSES, MODEL], U32, align_bytes=64)
        v_scales = keep.tile([P, KEY_PASSES, MODEL], U8, align_bytes=64)

        kv_grouped = keep.tile([P, BLOCKS, FEATURE_PASSES, P, 2], F32, align_bytes=64)
        kv_codes = keep.tile([P, BLOCKS, FEATURE_PASSES * P], U32, align_bytes=64)
        kv_scales = keep.tile([P, BLOCKS, FEATURE_PASSES * P], U8, align_bytes=64)
        w_grouped = keep.tile([P, FEATURE_PASSES, MODEL, PACK], BF16, align_bytes=64, tag="grouped")
        w_codes = keep.tile([P, FEATURE_PASSES, MODEL], U32, align_bytes=64)
        w_scales = keep.tile([P, FEATURE_PASSES, MODEL], U8, align_bytes=64)
        kv_words = kv_rows[:].bitcast(F32)
        def transpose_rows(h, src, dst, blocks=(0, BLOCKS), tag="work", on_scalar=True):
            lo, hi = blocks
            flipped = psum.tile([P, BLOCKS, P], BF16, tag=tag)
            for b in range(lo, hi):
                nc.tensor.transpose(out=flipped[:, b - lo, :], in_=src[:, h, b, :], identity=ident_bf[:])
            copy_out(on_scalar, dst[:, h, lo * P : hi * P], flipped[:, : hi - lo, :].rearrange("p b i -> p (b i)"))

        def live_blocks(ib):
            if ib == BLOCKS - 1:
                return list(range(BLOCKS))
            return [(ib + 2 + slot) % BLOCKS for slot in range(BLOCKS - 1)]

        def ring_start(ib):
            return (ib + 2 - ib % 2) % BLOCKS

        def first_live(ib):
            return P if ib % 2 == 1 and ib != BLOCKS - 1 else 0

        def bank_widths(ib):
            return (BANK, (len(live_blocks(ib)) - BANK_BLOCKS) * P)

        banks_of = {}
        neg_s_of = {}
        flipped_of = {}
        grouped_of = {}
        v_grouped_of = {}
        projected_of = {}

        def scores(n, c):
            h, ib = divmod(n, BLOCKS)
            bank = psum.tile([P, BANK], F32, tag=("s_lo", "s_hi")[c])
            banks_of[n, c] = bank
            for slot, jb in enumerate(live_blocks(ib)[c * BANK_BLOCKS : (c + 1) * BANK_BLOCKS]):
                dst = bank[:, slot * P : (slot + 1) * P]
                partly = jb == ib or jb == ib + 2
                nc.tensor.matmul(
                    out=dst, lhsT=qT[:, h, ib * P : (ib + 1) * P], rhs=kT[:, h, jb * P : (jb + 1) * P],
                    start=True, stop=not partly,
                )
                if partly:
                    nc.tensor.matmul(
                        out=dst, lhsT=ident_bf[:], rhs=band[:, 0 if jb == ib else 1, :], start=False, stop=True
                    )

        def shift_out(n, c):
            h, ib = divmod(n, BLOCKS)
            if c == 0:
                neg_s = wide.tile([P, SEQ], F32)
                first_min = small.tile([P, 1], F32)
                neg_s_of[n] = (neg_s, first_min)
            neg_s, first_min = neg_s_of[n]
            width = bank_widths(ib)[c]
            nc.vector.tensor_scalar(
                out=neg_s[:, c * BANK : c * BANK + width], in0=banks_of[n, c][:, :width], scalar1=-SCALE,
                scalar2=(neg_sink[:, h : h + 1], first_min[:])[c], op0=ALU.mult, op1=ALU.min,
                accum_out=(first_min[:], neg_max[:, n : n + 1])[c],
            )

        def exponentials(n):
            ib = n % BLOCKS
            width = sum(bank_widths(ib))
            nc.scalar.activation(
                out=e_rows_of[n // BLOCKS % 2][:, ib, first_live(ib) : first_live(ib) + width],
                in_=neg_s_of[n][0][:, :width], func=ACT.Exp,
                bias=neg_max[:, n : n + 1], scale=-1.0, accum_out=row_sums[:, n : n + 1],
            )

        def sink_terms(h):
            cols = slice(h * BLOCKS, (h + 1) * BLOCKS)
            nc.scalar.activation(
                out=sink_e[:, cols], in_=neg_max[:, cols], func=ACT.Exp, bias=sink[:, h : h + 1], scale=1.0
            )

        def denominators(h):
            cols = slice(h * BLOCKS, (h + 1) * BLOCKS)
            nc.vector.tensor_add(out=den[:, cols], in0=row_sums[:, cols], in1=sink_e[:, cols])

        def invert(h):
            cols = slice(h * BLOCKS, (h + 1) * BLOCKS)
            nc.vector.reciprocal(out=inv_den[:, cols], in_=den[:, cols])

        def flip(n, tag="eT"):
            ib = n % BLOCKS
            eT = psum.tile([P, BLOCKS // 2, P], F32, tag=tag)
            flipped_of[n] = eT
            e_words = e_rows_of[n // BLOCKS % 2][:].bitcast(F32)
            for place in range(BLOCKS // 2):
                a = (ring_start(ib) // 2 + place) % (BLOCKS // 2)
                nc.tensor.transpose(
                    out=eT[:, a, :], in_=e_words[:, ib, place * P : (place + 1) * P], identity=ident_f32[:]
                )

        def unload(n, on_scalar):
            if n % 2 == 0:
                grouped = stage.tile([P, 2, KEY_PASSES, P, 2], F32, align_bytes=64, bufs=2)
                grouped_of[n // 2] = grouped
            copy_out(on_scalar, grouped_of[n // 2][:, n % 2], flipped_of[n][:].rearrange("p (g u) i -> p g i u", u=2))

        def quantise_e(pair):
            nc.vector.quantize_mx(
                out=e_codes[:, 2 * pair : 2 * pair + 2, :].rearrange("p r w -> p (r w)").bitcast(FP8X4),
                scales=e_scales[:, 2 * pair : 2 * pair + 2, :].rearrange("p r w -> p (r w)"),
                in_=grouped_of[pair][:].bitcast(BF16).rearrange("p r g i t -> p (r g i t)"),
            )

        def regroup_w(piece):
            g, c = divmod(piece, MODEL // BANK)
            cols = slice(c * BANK, (c + 1) * BANK)
            nc.gpsimd.tensor_scalar(
                out=w_grouped[:, g, cols, :], in0=w_rows[:, g, :, cols].rearrange("p t n -> p n t"),
                scalar1=1.0, scalar2=0.0, op0=ALU.mult, op1=ALU.add,
            )

        def quantise_w(g):
            nc.vector.quantize_mx(
                out=w_codes[:, g, :].bitcast(FP8X4),
                scales=w_scales[:, g, :],
                in_=w_grouped[:, g].rearrange("p n t -> p (n t)"),
            )

        def flip_kv(jb):
            flipped = psum.tile([P, FEATURE_PASSES * 2, P], F32, tag="work")
            for a in range(FEATURE_PASSES * 2):
                nc.tensor.transpose(
                    out=flipped[:, a, :], in_=kv_words[:, jb, a * P : (a + 1) * P], identity=ident_f32[:]
                )
            nc.scalar.copy(out=kv_grouped[:, jb], in_=flipped[:].rearrange("p (g u) j -> p g j u", u=2))

        def quantise_kv(two):
            blocks = slice(2 * two, 2 * two + 2)
            nc.vector.quantize_mx(
                out=kv_codes[:, blocks, :].rearrange("p b w -> p (b w)").bitcast(FP8X4),
                scales=kv_scales[:, blocks, :].rearrange("p b w -> p (b w)"),
                in_=kv_grouped[:].bitcast(BF16)[:, blocks].rearrange("p b g j t -> p (b g j t)"),
            )

        def project(step):
            kp, nb = divmod(step, MODEL // P)
            cols = slice(nb * P, (nb + 1) * P)
            if step == 0:
                v_grouped = keep.tile([P, KEY_PASSES, MODEL, PACK], BF16, align_bytes=64, tag="grouped")
                v_grouped_of[0] = v_grouped
            acc = psum.tile([P, PACK, P], F32, tag="work")
            for t in range(PACK):
                jb = kp * PACK + t
                for g in range(FEATURE_PASSES):
                    nc.tensor.matmul_mx(
                        out=acc[:, t, :],
                        lhsT=kv_codes[:, jb, g * P : (g + 1) * P].bitcast(FP8X4),
                        lhsT_scale=kv_scales[:, jb, g * P : (g + 1) * P],
                        rhs=w_codes[:, g, cols].bitcast(FP8X4),
                        rhs_scale=w_scales[:, g, cols],
                        start=(g == 0),
                        stop=(g == FEATURE_PASSES - 1),
                    )
            projected_of[step] = acc

        def unload_v(step):
            kp, nb = divmod(step, MODEL // P)
            cols = slice(nb * P, (nb + 1) * P)
            nc.scalar.copy(
                out=v_grouped_of[0][:, kp, cols, :], in_=projected_of[step][:].rearrange("p t c -> p c t")
            )

        def quantise_v(kp):
            nc.vector.quantize_mx(
                out=v_codes[:, kp, :].bitcast(FP8X4),
                scales=v_scales[:, kp, :],
                in_=v_grouped_of[0][:, kp].rearrange("p n t -> p (n t)"),
            )

        acc_of = {}

        def weigh(pair, tag):
            h = 2 * pair // BLOCKS
            acc = psum.tile([P, 2, VALUE_DIM], F32, tag=tag)
            acc_of[pair] = acc
            cols = slice(h * VALUE_DIM, (h + 1) * VALUE_DIM)
            for r in range(2):
                n = 2 * pair + r
                for kp in range(KEY_PASSES):
                    nc.tensor.matmul_mx(
                        out=acc[:, r, :],
                        lhsT=e_codes[:, n, kp * P : (kp + 1) * P].bitcast(FP8X4),
                        lhsT_scale=e_scales[:, n, kp * P : (kp + 1) * P],
                        rhs=v_codes[:, kp, cols].bitcast(FP8X4),
                        rhs_scale=v_scales[:, kp, cols],
                        start=(kp == 0),
                        stop=(kp == KEY_PASSES - 1),
                    )

        def finish(pair):
            h, first = divmod(2 * pair, BLOCKS)
            result = stage.tile([P, 2, VALUE_DIM], F32, bufs=8)
            for r in range(2):
                n = 2 * pair + r
                nc.scalar.activation(
                    out=result[:, r, :], in_=acc_of[pair][:, r, :], func=ACT.Silu, scale=inv_den[:, n : n + 1]
                )
                nc.sync.dma_start(out=out[0, h, (first + r) * P : (first + r + 1) * P, :], in_=result[:, r, :])

        attended = []

        def attend(upto, ready):
            while len(attended) < min(upto, ready):
                pair = len(attended)
                if pair >= EARLY:
                    weigh(pair, ("work", "s_hi")[pair // 2 % 2])
                finish(pair)
                attended.append(pair)

        def tail_tag(n):
            return ("eT", "s_lo")[(n - (TILES - LAG)) // 2 % 2]

        transpose_rows(0, q_rows, qT, (0, FIRST_Q), "work", False)
        transpose_rows(0, k_rows, kT, (0, BLOCKS // 2), "eT", True)
        transpose_rows(0, k_rows, kT, (BLOCKS // 2, BLOCKS), "eT", False)
        for n in range(2):
            scores(n, 0)
            scores(n, 1)
        transpose_rows(0, q_rows, qT, (FIRST_Q, BLOCKS))
        shift_out(0, 0)
        scores(2, 0)
        shift_out(1, 0)
        shift_out(0, 1)
        for i in range(TILES):
            h, ib = divmod(i, BLOCKS)
            packed = i - LAG
            step = i - V_FIRST
            if i + 2 < TILES:
                scores(i + 2, 1)
            if i + 2 < TILES:
                shift_out(i + 2, 0)
            if packed >= 0:
                unload(packed, packed % 2 == 1 or i >= V_FIRST + KEY_PASSES * BLOCKS)
            if packed >= 3 and packed % 2 == 1:
                quantise_e((packed - 3) // 2)
            if i + 1 < TILES:
                shift_out(i + 1, 1)
            exponentials(i)
            if 0 < step <= KEY_PASSES * BLOCKS:
                unload_v(step - 1)
            if ib == 3 and h < HEADS - 1:
                transpose_rows(h + 1, q_rows, qT)
            if ib == 4 and h < HEADS - 1:
                transpose_rows(h + 1, k_rows, kT)
            if W_FIRST <= i < W_FIRST + 4:
                regroup_w(i - W_FIRST)
            if i == W_FIRST + 4:
                make_e_rows(1, "w_then_e", nc.gpsimd)
            if i in (W_QUANTISE, W_QUANTISE + 2):
                quantise_w((i - W_QUANTISE) // 2)
            if KV_FIRST < i <= KV_FIRST + BLOCKS and (i - KV_FIRST) % 2 == 0:
                quantise_kv((i - KV_FIRST) // 2 - 1)
            if KV_FIRST <= i < KV_FIRST + BLOCKS:
                flip_kv(i - KV_FIRST)
            if step > 1 and (step - 1) % BLOCKS == 0:
                quantise_v((step - 1) // BLOCKS - 1)
            if packed + 1 >= 0:
                flip(packed + 1)
            if i + 3 < TILES:
                scores(i + 3, 0)
            if 0 <= step < KEY_PASSES * BLOCKS:
                project(step)
            if i >= TILES - EARLY:
                weigh(i - (TILES - EARLY), "work")
            if ib == BLOCKS - 1:
                sink_terms(h)
            if ib == 1 and h > 0:
                denominators(h - 1)
            if ib == 2 and h > 0:
                invert(h - 1)
        first = TILES - LAG
        flip(first + 1)
        for a in range(first, TILES, 2):
            if a + 2 < TILES:
                flip(a + 2, tail_tag(a + 2))
                flip(a + 3, tail_tag(a + 3))
            unload(a, False)
            quantise_e(a // 2 - 1)
            unload(a + 1, False)
            if a == first:
                denominators(HEADS - 1)
            if a == first + 2:
                invert(HEADS - 1)
            attend((a + 2 - first) * (TILES // 2) // LAG + 1, a // 2)
        quantise_e(TILES // 2 - 1)
        attend(TILES // 2, TILES // 2)
